import numpy as np
import ml_dtypes


def mxq(x, axis, fmt="e4m3"):
    dtype, down = {"e4m3": (ml_dtypes.float8_e4m3fn, 7), "e5m2": (ml_dtypes.float8_e5m2, 14)}[fmt]
    v = np.moveaxis(np.asarray(x, np.float32).astype(ml_dtypes.bfloat16).astype(np.float64), axis, -1)
    blocks = v.reshape(v.shape[:-1] + (-1, 32))
    amax = np.abs(blocks).max(-1, keepdims=True)
    byte = np.maximum(np.where(amax > 0, np.frexp(amax)[1] - 1 + 127, 0) - down, 1)
    scale = np.exp2(byte - 127.0)
    codes = (blocks / scale).astype(np.float32).astype(dtype).astype(np.float64)
    return np.moveaxis((codes * scale).reshape(v.shape), -1, axis)


WIDE = False


def mx_kscale(k):
    if not WIDE:
        return np.ones(k)
    levels = np.array([10, -10, 5, -5, 0])
    a = np.random.permutation(np.resize(levels, k // 512 * 4)).reshape(k // 512, 4)
    idx = np.arange(k)
    return np.exp2(a[idx // 512, idx % 128 // 32])


BF16 = ml_dtypes.bfloat16


def bf(x):
    return np.asarray(x, np.float32).astype(BF16)


def f64(x):
    return np.asarray(x).astype(np.float64)


E2M1 = np.array([0.0, 0.5, 1.0, 1.5, 2.0, 3.0, 4.0, 6.0, -0.0, -0.5, -1.0, -1.5, -2.0, -3.0, -4.0, -6.0])


def pack_weight(w, fmt):
    k, n = w.shape
    w = f64(bf(w)).reshape(k // 32, 32, n)
    amax = np.abs(w).max(1)
    if fmt == "e4m3":
        byte = np.frexp(amax)[1] - 1 + 127 - 7
    else:
        mant, ex = np.frexp(amax / 6.0)
        byte = np.where(mant > 0.5, ex, ex - 1) + 127
    byte = np.clip(np.where(amax > 0, byte, 1), 1, 254)
    scaled = (w * np.exp2(127.0 - byte)[:, None, :]).reshape(k, n).astype(np.float32)
    by_word = np.ascontiguousarray(scaled.reshape(k // 512, 128, 4, n).transpose(0, 1, 3, 2))
    if fmt == "e4m3":
        words = by_word.astype(ml_dtypes.float8_e4m3fn).view(np.uint8)
    else:
        c = by_word.astype(ml_dtypes.float4_e2m1fn).view(np.uint8) & 0xF
        words = c[..., 0::2] | (c[..., 1::2] << 4)
    return np.ascontiguousarray(words), np.ascontiguousarray(byte.astype(np.uint8).reshape(k // 512, 16, n))


def unpack_weight(words, scales, fmt):
    g, p, n, _ = words.shape
    if fmt == "e4m3":
        vals = np.ascontiguousarray(words).view(ml_dtypes.float8_e4m3fn).astype(np.float64)
    else:
        nib = np.empty((g, p, n, 4), np.uint8)
        nib[..., 0::2] = words & 0xF
        nib[..., 1::2] = words >> 4
        vals = E2M1[nib]
    vals = vals * np.repeat(np.exp2(scales.astype(np.float64) - 127.0), 8, axis=1)[..., None]
    return vals.transpose(0, 1, 3, 2).reshape(g * 512, n)


B, D, H = 4096, 1024, 256
G = 4
QH = H % 512 == 0


def sigmoid(v):
    return 1.0 / (1.0 + np.exp(-v))


def setup_inputs():
    s = mx_kscale(D)
    t = mx_kscale(H) if QH else np.ones(H)
    x_t = bf(np.random.standard_normal((B, D)) * s)
    h_pre = bf(np.random.standard_normal((B, H)) * t)
    c_pre = bf(np.random.standard_normal((B, H)))
    Wx = np.random.standard_normal((G, H, D)) * 0.64 / np.sqrt(D) / s
    Wx_cat = np.ascontiguousarray(Wx.swapaxes(1, 2)).reshape(-1, H)
    Wx_words, Wx_scales = pack_weight(Wx_cat, "e4m3")
    bW = bf(np.random.standard_normal((4, H)) * 0.3)
    Uh = bf(np.random.standard_normal((4, H, H)) * 0.64 / np.sqrt(H) / t)
    bU = bf(np.random.standard_normal((4, H)) * 0.3)
    return {
        "x_t": x_t,
        "h_pre": h_pre,
        "c_pre": c_pre,
        "Wx_words": Wx_words,
        "Wx_scales": Wx_scales,
        "bW": bW,
        "Uh": Uh,
        "bU": bU,
    }


def reference(x_t, h_pre, c_pre, Wx_words, Wx_scales, bW, Uh, bU):
    zx = mxq(f64(x_t), 1, "e4m3") @ unpack_weight(Wx_words, Wx_scales, "e4m3").reshape(G, D, H)
    if QH:
        zh = mxq(f64(h_pre), 1, "e4m3") @ mxq(f64(Uh), 2, "e4m3").transpose(0, 2, 1)
    else:
        zh = f64(h_pre) @ f64(Uh).transpose(0, 2, 1)
    z = zx + zh + (f64(bW) + f64(bU))[:, None, :]
    f_t = sigmoid(z[0])
    i_t = sigmoid(z[1])
    o_t = sigmoid(z[2])
    g_t = np.tanh(z[3])
    c_t = f_t * f64(c_pre) + i_t * g_t
    h_t = o_t * np.tanh(c_t)
    return (h_t, c_t)

@@ -1,0 +1,194 @@
+from contextlib import ExitStack
+
+import concourse.mybir as mybir
+from concourse.masks import make_identity
+
+F32 = mybir.dt.float32
+BF16 = mybir.dt.bfloat16
+I32 = mybir.dt.int32
+U32 = mybir.dt.uint32
+U8 = mybir.dt.uint8
+FP8X4 = mybir.dt.float8_e4m3fn_x4
+ACT = mybir.ActivationFunctionType
+ALU = mybir.AluOpType
+
+B, D, H, GATES = 4096, 1024, 256, 4
+FLOPS = 2 * B * D * GATES * H + 2 * B * H * GATES * H
+
+P = 128
+PACK = 4
+K_PASS = P * PACK
+X_PASSES = D // K_PASS
+H_PASSES = H // P
+Z = GATES * H
+N_TILE = 512
+HALVES = Z // N_TILE
+ROW_TILES = 2
+BLOCK = ROW_TILES * P
+BLOCKS = B // BLOCK
+
+
+def tile_lstmcell_t_e_kernel(tc, x_t, h_pre, c_pre, Wx_words, Wx_scales, bW, Uh, bU, out_0, out_1):
+    nc = tc.nc
+    with ExitStack() as ctx:
+        const = ctx.enter_context(tc.tile_pool(name="const", bufs=1))
+        inputs = ctx.enter_context(tc.tile_pool(name="inputs", bufs=BLOCKS))
+        work = ctx.enter_context(tc.tile_pool(name="work", bufs=3))
+        psum_t = ctx.enter_context(tc.psum_pool(name="psum_t", bufs=1))
+        psum_z = ctx.enter_context(tc.psum_pool(name="psum_z", bufs=5))
+
+        x_sb, h_sb, c_sb = [], [], []
+
+        def load_block(b):
+            rows = slice(b * BLOCK, (b + 1) * BLOCK)
+            x_blk = inputs.tile([P, ROW_TILES, D], BF16, name="x_blk")
+            nc.sync.dma_start(out=x_blk[:], in_=x_t[rows, :].rearrange("(p t) d -> p t d", t=ROW_TILES))
+            h_blk = inputs.tile([P, ROW_TILES, H], BF16, name="h_blk")
+            nc.sync.dma_start(out=h_blk[:], in_=h_pre[rows, :].rearrange("(p t) d -> p t d", t=ROW_TILES))
+            c_blk = inputs.tile([P, ROW_TILES, H], BF16, name="c_blk")
+            nc.sync.dma_start(out=c_blk[:], in_=c_pre[rows, :].rearrange("(p t) d -> p t d", t=ROW_TILES))
+            x_sb.append(x_blk)
+            h_sb.append(h_blk)
+            c_sb.append(c_blk)
+
+        w_scales = const.tile([P, X_PASSES, Z], U8, align_bytes=64)
+        nc.vector.memset(w_scales[:].rearrange("p c n -> p (c n)").bitcast(I32), 0)
+        bias_rows = const.tile([P, Z], BF16)
+        nc.vector.memset(bias_rows[:], 0.0)
+        ones = const.tile([P, P], BF16)
+        nc.vector.memset(ones[:], 1.0)
+        ident_f32 = const.tile([P, P], F32)
+        make_identity(nc, ident_f32[:])
+        ident_bf16 = const.tile([P, P], BF16)
+        make_identity(nc, ident_bf16[:])
+
+        load_block(0)
+
+        scale_words = Wx_scales.bitcast(I32).rearrange("(e c) q n -> c q e n", c=X_PASSES)
+        for c in range(X_PASSES):
+            for quad in range(4):
+                nc.sync.dma_start(
+                    out=w_scales[32 * quad : 32 * quad + 4, c, :].bitcast(I32).rearrange("q (e n) -> q e n", e=GATES),
+                    in_=scale_words[c, 4 * quad : 4 * quad + 4],
+                )
+        uh_sb = const.tile([P, Z // P, H], BF16)
+        nc.sync.dma_start(out=uh_sb[:], in_=Uh.rearrange("e (a p) k -> p (e a) k", p=P))
+        nc.sync.dma_start(out=bias_rows[0:1, :], in_=bW.rearrange("(o e) n -> o (e n)", o=1))
+        nc.sync.dma_start(out=bias_rows[1:2, :], in_=bU.rearrange("(o e) n -> o (e n)", o=1))
+        w_words = const.tile([P, X_PASSES, Z], U32, align_bytes=64)
+        code_words = Wx_words.rearrange("g p n t -> g p (n t)").bitcast(I32).rearrange("(e c) p n -> c p e n", c=X_PASSES)
+        for c in range(X_PASSES):
+            nc.sync.dma_start(
+                out=w_words[:, c, :].bitcast(I32).rearrange("p (e n) -> p e n", e=GATES),
+                in_=code_words[c],
+            )
+        for b in range(1, BLOCKS):
+            load_block(b)
+
+        x_codes, x_scales, hT_sb, z_sb, c_new = {}, {}, {}, {}, {}
+
+        def transpose_block(b):
+            grouped = work.tile([P, ROW_TILES, X_PASSES, P, PACK], BF16, align_bytes=64, name="grouped")
+            for t in range(ROW_TILES):
+                words = x_sb[b][:, t, :].bitcast(F32)
+                xT_ps = psum_t.tile([P, X_PASSES, 2, P], F32, name="xT_ps%d" % t)
+                for g in range(X_PASSES):
+                    for u in range(2):
+                        first = (K_PASS // 2) * g + u
+                        nc.tensor.transpose(xT_ps[:, g, u, :], words[:, first : (K_PASS // 2) * (g + 1) : 2], ident_f32[:])
+                nc.scalar.copy(out=grouped[:, t].bitcast(F32), in_=xT_ps[:].rearrange("p g u r -> p g r u"))
+            hT_ps = psum_t.tile([P, ROW_TILES, H_PASSES, P], BF16, name="hT_ps")
+            for t in range(ROW_TILES):
+                for kt in range(H_PASSES):
+                    nc.tensor.transpose(hT_ps[:, t, kt, :], h_sb[b][:, t, kt * P : (kt + 1) * P], ident_bf16[:])
+            hT = work.tile([P, ROW_TILES, H_PASSES, P], BF16, name="hT")
+            nc.scalar.copy(out=hT[:], in_=hT_ps[:])
+            codes = work.tile([P, ROW_TILES * X_PASSES * P], U32, align_bytes=64, name="codes")
+            scales = work.tile([P, ROW_TILES * X_PASSES * P], U8, align_bytes=64, name="scales")
+            nc.vector.quantize_mx(
+                out=codes[:].bitcast(FP8X4),
+                scales=scales[:],
+                in_=grouped[:].rearrange("p t g r k -> p (t g r k)"),
+            )
+            x_codes[b], x_scales[b], hT_sb[b] = codes, scales, hT
+
+        def matmul_block(b):
+            z = work.tile([P, ROW_TILES, Z], F32, name="z", bufs=4)
+            for t in range(ROW_TILES):
+                for half in range(HALVES):
+                    cols = slice(half * N_TILE, (half + 1) * N_TILE)
+                    zh_ps = psum_z.tile([P, N_TILE], F32, name="zh_ps", tag="z_ps")
+                    for kt in range(H_PASSES):
+                        nc.tensor.matmul(
+                            out=zh_ps[:],
+                            lhsT=hT_sb[b][:, t, kt, :],
+                            rhs=uT_sb[:, kt, cols],
+                            start=(kt == 0),
+                            stop=(kt == H_PASSES - 1),
+                        )
+                    zx_ps = psum_z.tile([P, N_TILE], F32, name="zx_ps", tag="z_ps")
+                    for g in range(X_PASSES):
+                        rows = slice((t * X_PASSES + g) * P, (t * X_PASSES + g + 1) * P)
+                        nc.tensor.matmul_mx(
+                            out=zx_ps[:],
+                            lhsT=x_codes[b][:, rows].bitcast(FP8X4),
+                            lhsT_scale=x_scales[b][:, rows],
+                            rhs=w_words[:, g, cols].bitcast(FP8X4),
+                            rhs_scale=w_scales[:, g, cols],
+                            start=(g == 0),
+                            stop=(g == X_PASSES - 1),
+                        )
+                    nc.vector.tensor_tensor(out=z[:, t, cols], in0=zh_ps[:], in1=bias_sb[:, cols], op=ALU.add)
+                    nc.vector.tensor_tensor(out=z[:, t, cols], in0=zx_ps[:], in1=z[:, t, cols], op=ALU.add)
+            z_sb[b] = z
+
+        def gates_block(b):
+            z = z_sb[b]
+            nc.scalar.activation(out=z[:, :, 0 : 3 * H], in_=z[:, :, 0 : 3 * H], func=ACT.Sigmoid)
+            nc.scalar.activation(out=z[:, :, 3 * H : Z], in_=z[:, :, 3 * H : Z], func=ACT.Tanh)
+
+        def cell_block(b):
+            z = z_sb[b]
+            fc = work.tile([P, ROW_TILES, H], F32, name="fc")
+            nc.gpsimd.tensor_tensor(out=fc[:], in0=z[:, :, 0:H], in1=c_sb[b][:], op=ALU.mult)
+            ig = work.tile([P, ROW_TILES, H], F32, name="ig")
+            nc.gpsimd.tensor_tensor(out=ig[:], in0=z[:, :, H : 2 * H], in1=z[:, :, 3 * H : Z], op=ALU.mult)
+            c_t = work.tile([P, ROW_TILES, H], F32, name="c_t")
+            nc.gpsimd.tensor_tensor(out=c_t[:], in0=fc[:], in1=ig[:], op=ALU.add)
+            c_new[b] = c_t
+
+        def hidden_block(b):
+            rows = slice(b * BLOCK, (b + 1) * BLOCK)
+            tanh_c = work.tile([P, ROW_TILES, H], F32, name="tanh_c")
+            nc.scalar.activation(out=tanh_c[:], in_=c_new[b][:], func=ACT.Tanh)
+            h_t = work.tile([P, ROW_TILES, H], F32, name="h_t")
+            nc.gpsimd.tensor_tensor(out=h_t[:], in0=z_sb[b][:, :, 2 * H : 3 * H], in1=tanh_c[:], op=ALU.mult)
+            nc.sync.dma_start(out=out_1[rows, :].rearrange("(p t) n -> p t n", t=ROW_TILES), in_=c_new[b][:])
+            nc.sync.dma_start(out=out_0[rows, :].rearrange("(p t) n -> p t n", t=ROW_TILES), in_=h_t[:])
+
+        ctx.enter_context(tc.manual_schedule())
+        transpose_block(0)
+
+        uT_sb = const.tile([P, H_PASSES, Z], BF16)
+        for kt in range(H_PASSES):
+            uT_ps = psum_z.tile([P, Z], BF16, name="uT_ps", tag="z_ps")
+            for a in range(Z // P):
+                nc.tensor.transpose(uT_ps[:, a * P : (a + 1) * P], uh_sb[:, a, kt * P : (kt + 1) * P], ident_bf16[:])
+            nc.scalar.copy(out=uT_sb[:, kt, :], in_=uT_ps[:])
+        bias_sb = const.tile([P, Z], F32)
+        for half in range(HALVES):
+            cols = slice(half * N_TILE, (half + 1) * N_TILE)
+            bias_ps = psum_z.tile([P, N_TILE], F32, name="bias_ps", tag="z_ps")
+            nc.tensor.matmul(out=bias_ps[:], lhsT=ones[:], rhs=bias_rows[:, cols], start=True, stop=True)
+            nc.vector.tensor_copy(out=bias_sb[:, cols], in_=bias_ps[:])
+
+        for step in range(1, BLOCKS + 3):
+            if step < BLOCKS:
+                transpose_block(step)
+            if 0 <= step - 1 < BLOCKS:
+                matmul_block(step - 1)
+            if 0 <= step - 2 < BLOCKS:
+                gates_block(step - 2)
+                cell_block(step - 2)
+            if 0 <= step - 3 < BLOCKS:
+                hidden_block(step - 3)

@@ -63,6 +63,11 @@ def tile_lstmcell_t_e_kernel(tc, x_t, h_pre, c_pre, Wx_words, Wx_scales, bW, Uh,
         make_identity(nc, ident_bf16[:])
 
         load_block(0)
+        uh_sb = const.tile([P, Z // P, H], BF16)
+        nc.sync.dma_start(out=uh_sb[:], in_=Uh.rearrange("e (a p) k -> p (e a) k", p=P))
+        nc.sync.dma_start(out=bias_rows[0:1, :], in_=bW.rearrange("(o e) n -> o (e n)", o=1))
+        nc.sync.dma_start(out=bias_rows[1:2, :], in_=bU.rearrange("(o e) n -> o (e n)", o=1))
+        load_block(1)
 
         scale_words = Wx_scales.bitcast(I32).rearrange("(e c) q n -> c q e n", c=X_PASSES)
         for c in range(X_PASSES):
@@ -71,10 +76,6 @@ def tile_lstmcell_t_e_kernel(tc, x_t, h_pre, c_pre, Wx_words, Wx_scales, bW, Uh,
                     out=w_scales[32 * quad : 32 * quad + 4, c, :].bitcast(I32).rearrange("q (e n) -> q e n", e=GATES),
                     in_=scale_words[c, 4 * quad : 4 * quad + 4],
                 )
-        uh_sb = const.tile([P, Z // P, H], BF16)
-        nc.sync.dma_start(out=uh_sb[:], in_=Uh.rearrange("e (a p) k -> p (e a) k", p=P))
-        nc.sync.dma_start(out=bias_rows[0:1, :], in_=bW.rearrange("(o e) n -> o (e n)", o=1))
-        nc.sync.dma_start(out=bias_rows[1:2, :], in_=bU.rearrange("(o e) n -> o (e n)", o=1))
         w_words = const.tile([P, X_PASSES, Z], U32, align_bytes=64)
         code_words = Wx_words.rearrange("g p n t -> g p (n t)").bitcast(I32).rearrange("(e c) p n -> c p e n", c=X_PASSES)
         for c in range(X_PASSES):
@@ -82,10 +83,10 @@ def tile_lstmcell_t_e_kernel(tc, x_t, h_pre, c_pre, Wx_words, Wx_scales, bW, Uh,
                 out=w_words[:, c, :].bitcast(I32).rearrange("p (e n) -> p e n", e=GATES),
                 in_=code_words[c],
             )
-        for b in range(1, BLOCKS):
+        for b in range(2, BLOCKS):
             load_block(b)
 
-        x_codes, x_scales, hT_sb, z_sb, c_new = {}, {}, {}, {}, {}
+        x_grouped, x_codes, x_scales, hT_sb, z_sb, products, c_new = {}, {}, {}, {}, {}, {}, {}
 
         def transpose_block(b):
             grouped = work.tile([P, ROW_TILES, X_PASSES, P, PACK], BF16, align_bytes=64, name="grouped")
@@ -103,58 +104,76 @@ def tile_lstmcell_t_e_kernel(tc, x_t, h_pre, c_pre, Wx_words, Wx_scales, bW, Uh,
                     nc.tensor.transpose(hT_ps[:, t, kt, :], h_sb[b][:, t, kt * P : (kt + 1) * P], ident_bf16[:])
             hT = work.tile([P, ROW_TILES, H_PASSES, P], BF16, name="hT")
             nc.scalar.copy(out=hT[:], in_=hT_ps[:])
+            x_grouped[b], hT_sb[b] = grouped, hT
+
+        def quantise_block(b):
             codes = work.tile([P, ROW_TILES * X_PASSES * P], U32, align_bytes=64, name="codes")
             scales = work.tile([P, ROW_TILES * X_PASSES * P], U8, align_bytes=64, name="scales")
             nc.vector.quantize_mx(
                 out=codes[:].bitcast(FP8X4),
                 scales=scales[:],
-                in_=grouped[:].rearrange("p t g r k -> p (t g r k)"),
+                in_=x_grouped[b][:].rearrange("p t g r k -> p (t g r k)"),
             )
-            x_codes[b], x_scales[b], hT_sb[b] = codes, scales, hT
+            x_codes[b], x_scales[b] = codes, scales
 
         def matmul_block(b):
             z = work.tile([P, ROW_TILES, Z], F32, name="z", bufs=4)
+            z_sb[b] = z
             for t in range(ROW_TILES):
+                halves = [slice(half * N_TILE, (half + 1) * N_TILE) for half in range(HALVES)]
+                zh_ps = [psum_z.tile([P, N_TILE], F32, name="zh_ps", tag="z_ps") for half in range(HALVES)]
                 for half in range(HALVES):
-                    cols = slice(half * N_TILE, (half + 1) * N_TILE)
-                    zh_ps = psum_z.tile([P, N_TILE], F32, name="zh_ps", tag="z_ps")
                     for kt in range(H_PASSES):
                         nc.tensor.matmul(
-                            out=zh_ps[:],
+                            out=zh_ps[half][:],
                             lhsT=hT_sb[b][:, t, kt, :],
-                            rhs=uT_sb[:, kt, cols],
+                            rhs=uT_sb[:, kt, halves[half]],
                             start=(kt == 0),
                             stop=(kt == H_PASSES - 1),
                         )
-                    zx_ps = psum_z.tile([P, N_TILE], F32, name="zx_ps", tag="z_ps")
+                zx_ps = [psum_z.tile([P, N_TILE], F32, name="zx_ps", tag="z_ps") for half in range(HALVES)]
+                for half in range(HALVES):
                     for g in range(X_PASSES):
                         rows = slice((t * X_PASSES + g) * P, (t * X_PASSES + g + 1) * P)
                         nc.tensor.matmul_mx(
-                            out=zx_ps[:],
+                            out=zx_ps[half][:],
                             lhsT=x_codes[b][:, rows].bitcast(FP8X4),
                             lhsT_scale=x_scales[b][:, rows],
-                            rhs=w_words[:, g, cols].bitcast(FP8X4),
-                            rhs_scale=w_scales[:, g, cols],
+                            rhs=w_words[:, g, halves[half]].bitcast(FP8X4),
+                            rhs_scale=w_scales[:, g, halves[half]],
                             start=(g == 0),
                             stop=(g == X_PASSES - 1),
                         )
-                    nc.vector.tensor_tensor(out=z[:, t, cols], in0=zh_ps[:], in1=bias_sb[:, cols], op=ALU.add)
-                    nc.vector.tensor_tensor(out=z[:, t, cols], in0=zx_ps[:], in1=z[:, t, cols], op=ALU.add)
-            z_sb[b] = z
+                for half in range(HALVES):
+                    nc.vector.tensor_tensor(out=z[:, t, halves[half]], in0=zh_ps[half][:], in1=bias_sb[:, halves[half]], op=ALU.add)
+                for half in range(HALVES):
+                    nc.vector.tensor_tensor(out=z[:, t, halves[half]], in0=zx_ps[half][:], in1=z[:, t, halves[half]], op=ALU.add)
+                if t == 0 and b + 1 < BLOCKS:
+                    quantise_block(b + 1)
 
         def gates_block(b):
             z = z_sb[b]
-            nc.scalar.activation(out=z[:, :, 0 : 3 * H], in_=z[:, :, 0 : 3 * H], func=ACT.Sigmoid)
-            nc.scalar.activation(out=z[:, :, 3 * H : Z], in_=z[:, :, 3 * H : Z], func=ACT.Tanh)
+            for t in range(ROW_TILES):
+                nc.scalar.activation(out=z[:, t, 0 : 3 * H], in_=z[:, t, 0 : 3 * H], func=ACT.Sigmoid)
+                nc.scalar.activation(out=z[:, t, 3 * H : Z], in_=z[:, t, 3 * H : Z], func=ACT.Tanh)
 
-        def cell_block(b):
+        def elementwise_engine(b):
+            return nc.vector if b == BLOCKS - 1 else nc.gpsimd
+
+        def cell_products(b):
             z = z_sb[b]
             fc = work.tile([P, ROW_TILES, H], F32, name="fc")
-            nc.gpsimd.tensor_tensor(out=fc[:], in0=z[:, :, 0:H], in1=c_sb[b][:], op=ALU.mult)
+            elementwise_engine(b).tensor_tensor(out=fc[:], in0=z[:, :, 0:H], in1=c_sb[b][:], op=ALU.mult)
             ig = work.tile([P, ROW_TILES, H], F32, name="ig")
-            nc.gpsimd.tensor_tensor(out=ig[:], in0=z[:, :, H : 2 * H], in1=z[:, :, 3 * H : Z], op=ALU.mult)
+            elementwise_engine(b).tensor_tensor(out=ig[:], in0=z[:, :, H : 2 * H], in1=z[:, :, 3 * H : Z], op=ALU.mult)
+            products[b] = (fc, ig)
+
+        def cell_sum(b):
+            rows = slice(b * BLOCK, (b + 1) * BLOCK)
+            fc, ig = products[b]
             c_t = work.tile([P, ROW_TILES, H], F32, name="c_t")
-            nc.gpsimd.tensor_tensor(out=c_t[:], in0=fc[:], in1=ig[:], op=ALU.add)
+            elementwise_engine(b).tensor_tensor(out=c_t[:], in0=fc[:], in1=ig[:], op=ALU.add)
+            nc.sync.dma_start(out=out_1[rows, :].rearrange("(p t) n -> p t n", t=ROW_TILES), in_=c_t[:])
             c_new[b] = c_t
 
         def hidden_block(b):
@@ -162,12 +181,12 @@ def tile_lstmcell_t_e_kernel(tc, x_t, h_pre, c_pre, Wx_words, Wx_scales, bW, Uh,
             tanh_c = work.tile([P, ROW_TILES, H], F32, name="tanh_c")
             nc.scalar.activation(out=tanh_c[:], in_=c_new[b][:], func=ACT.Tanh)
             h_t = work.tile([P, ROW_TILES, H], F32, name="h_t")
-            nc.gpsimd.tensor_tensor(out=h_t[:], in0=z_sb[b][:, :, 2 * H : 3 * H], in1=tanh_c[:], op=ALU.mult)
-            nc.sync.dma_start(out=out_1[rows, :].rearrange("(p t) n -> p t n", t=ROW_TILES), in_=c_new[b][:])
+            elementwise_engine(b).tensor_tensor(out=h_t[:], in0=z_sb[b][:, :, 2 * H : 3 * H], in1=tanh_c[:], op=ALU.mult)
             nc.sync.dma_start(out=out_0[rows, :].rearrange("(p t) n -> p t n", t=ROW_TILES), in_=h_t[:])
 
         ctx.enter_context(tc.manual_schedule())
         transpose_block(0)
+        quantise_block(0)
 
         uT_sb = const.tile([P, H_PASSES, Z], BF16)
         for kt in range(H_PASSES):
@@ -189,6 +208,8 @@ def tile_lstmcell_t_e_kernel(tc, x_t, h_pre, c_pre, Wx_words, Wx_scales, bW, Uh,
                 matmul_block(step - 1)
             if 0 <= step - 2 < BLOCKS:
                 gates_block(step - 2)
-                cell_block(step - 2)
+                cell_products(step - 2)
             if 0 <= step - 3 < BLOCKS:
                 hidden_block(step - 3)
+            if 0 <= step - 2 < BLOCKS:
+                cell_sum(step - 2)

@@ -39,16 +39,19 @@ def tile_lstmcell_t_e_kernel(tc, x_t, h_pre, c_pre, Wx_words, Wx_scales, bW, Uh,
 
         x_sb, h_sb, c_sb = [], [], []
 
-        def load_block(b):
+        def load_x_h(b):
             rows = slice(b * BLOCK, (b + 1) * BLOCK)
             x_blk = inputs.tile([P, ROW_TILES, D], BF16, name="x_blk")
             nc.sync.dma_start(out=x_blk[:], in_=x_t[rows, :].rearrange("(p t) d -> p t d", t=ROW_TILES))
             h_blk = inputs.tile([P, ROW_TILES, H], BF16, name="h_blk")
             nc.sync.dma_start(out=h_blk[:], in_=h_pre[rows, :].rearrange("(p t) d -> p t d", t=ROW_TILES))
-            c_blk = inputs.tile([P, ROW_TILES, H], BF16, name="c_blk")
-            nc.sync.dma_start(out=c_blk[:], in_=c_pre[rows, :].rearrange("(p t) d -> p t d", t=ROW_TILES))
             x_sb.append(x_blk)
             h_sb.append(h_blk)
+
+        def load_c(b):
+            rows = slice(b * BLOCK, (b + 1) * BLOCK)
+            c_blk = inputs.tile([P, ROW_TILES, H], BF16, name="c_blk")
+            nc.sync.dma_start(out=c_blk[:], in_=c_pre[rows, :].rearrange("(p t) d -> p t d", t=ROW_TILES))
             c_sb.append(c_blk)
 
         w_scales = const.tile([P, X_PASSES, Z], U8, align_bytes=64)
@@ -62,12 +65,12 @@ def tile_lstmcell_t_e_kernel(tc, x_t, h_pre, c_pre, Wx_words, Wx_scales, bW, Uh,
         ident_bf16 = const.tile([P, P], BF16)
         make_identity(nc, ident_bf16[:])
 
-        load_block(0)
+        load_x_h(0)
         uh_sb = const.tile([P, Z // P, H], BF16)
         nc.sync.dma_start(out=uh_sb[:], in_=Uh.rearrange("e (a p) k -> p (e a) k", p=P))
         nc.sync.dma_start(out=bias_rows[0:1, :], in_=bW.rearrange("(o e) n -> o (e n)", o=1))
         nc.sync.dma_start(out=bias_rows[1:2, :], in_=bU.rearrange("(o e) n -> o (e n)", o=1))
-        load_block(1)
+        load_x_h(1)
 
         scale_words = Wx_scales.bitcast(I32).rearrange("(e c) q n -> c q e n", c=X_PASSES)
         for c in range(X_PASSES):
@@ -84,19 +87,29 @@ def tile_lstmcell_t_e_kernel(tc, x_t, h_pre, c_pre, Wx_words, Wx_scales, bW, Uh,
                 in_=code_words[c],
             )
         for b in range(2, BLOCKS):
-            load_block(b)
+            load_x_h(b)
+            load_c(b - 2)
+        load_c(BLOCKS - 2)
+        load_c(BLOCKS - 1)
 
-        x_grouped, x_codes, x_scales, hT_sb, z_sb, products, c_new = {}, {}, {}, {}, {}, {}, {}
+        x_sorted, x_grouped, x_codes, x_scales, hT_sb, z_sb, c_new, tanh_new = {}, {}, {}, {}, {}, {}, {}, {}
+
+        def sort_block(b):
+            in_order = work.tile([P, ROW_TILES, X_PASSES, 2, P], F32, name="in_order")
+            for t in range(ROW_TILES):
+                nc.scalar.copy(
+                    out=in_order[:, t],
+                    in_=x_sb[b][:, t, :].bitcast(F32).rearrange("p (g j u) -> p g u j", g=X_PASSES, u=2),
+                )
+            x_sorted[b] = in_order
 
         def transpose_block(b):
             grouped = work.tile([P, ROW_TILES, X_PASSES, P, PACK], BF16, align_bytes=64, name="grouped")
             for t in range(ROW_TILES):
-                words = x_sb[b][:, t, :].bitcast(F32)
                 xT_ps = psum_t.tile([P, X_PASSES, 2, P], F32, name="xT_ps%d" % t)
                 for g in range(X_PASSES):
                     for u in range(2):
-                        first = (K_PASS // 2) * g + u
-                        nc.tensor.transpose(xT_ps[:, g, u, :], words[:, first : (K_PASS // 2) * (g + 1) : 2], ident_f32[:])
+                        nc.tensor.transpose(xT_ps[:, g, u, :], x_sorted[b][:, t, g, u, :], ident_f32[:])
                 nc.scalar.copy(out=grouped[:, t].bitcast(F32), in_=xT_ps[:].rearrange("p g u r -> p g r u"))
             hT_ps = psum_t.tile([P, ROW_TILES, H_PASSES, P], BF16, name="hT_ps")
             for t in range(ROW_TILES):
@@ -116,40 +129,38 @@ def tile_lstmcell_t_e_kernel(tc, x_t, h_pre, c_pre, Wx_words, Wx_scales, bW, Uh,
             )
             x_codes[b], x_scales[b] = codes, scales
 
-        def matmul_block(b):
-            z = work.tile([P, ROW_TILES, Z], F32, name="z", bufs=4)
-            z_sb[b] = z
-            for t in range(ROW_TILES):
-                halves = [slice(half * N_TILE, (half + 1) * N_TILE) for half in range(HALVES)]
-                zh_ps = [psum_z.tile([P, N_TILE], F32, name="zh_ps", tag="z_ps") for half in range(HALVES)]
-                for half in range(HALVES):
-                    for kt in range(H_PASSES):
-                        nc.tensor.matmul(
-                            out=zh_ps[half][:],
-                            lhsT=hT_sb[b][:, t, kt, :],
-                            rhs=uT_sb[:, kt, halves[half]],
-                            start=(kt == 0),
-                            stop=(kt == H_PASSES - 1),
-                        )
-                zx_ps = [psum_z.tile([P, N_TILE], F32, name="zx_ps", tag="z_ps") for half in range(HALVES)]
-                for half in range(HALVES):
-                    for g in range(X_PASSES):
-                        rows = slice((t * X_PASSES + g) * P, (t * X_PASSES + g + 1) * P)
-                        nc.tensor.matmul_mx(
-                            out=zx_ps[half][:],
-                            lhsT=x_codes[b][:, rows].bitcast(FP8X4),
-                            lhsT_scale=x_scales[b][:, rows],
-                            rhs=w_words[:, g, halves[half]].bitcast(FP8X4),
-                            rhs_scale=w_scales[:, g, halves[half]],
-                            start=(g == 0),
-                            stop=(g == X_PASSES - 1),
-                        )
-                for half in range(HALVES):
-                    nc.vector.tensor_tensor(out=z[:, t, halves[half]], in0=zh_ps[half][:], in1=bias_sb[:, halves[half]], op=ALU.add)
-                for half in range(HALVES):
-                    nc.vector.tensor_tensor(out=z[:, t, halves[half]], in0=zx_ps[half][:], in1=z[:, t, halves[half]], op=ALU.add)
-                if t == 0 and b + 1 < BLOCKS:
-                    quantise_block(b + 1)
+        def matmul_row_tile(b, t):
+            if t == 0:
+                z_sb[b] = work.tile([P, ROW_TILES, Z], F32, name="z", bufs=4)
+            z = z_sb[b]
+            halves = [slice(half * N_TILE, (half + 1) * N_TILE) for half in range(HALVES)]
+            zh_ps = [psum_z.tile([P, N_TILE], F32, name="zh_ps", tag="z_ps") for half in range(HALVES)]
+            for half in range(HALVES):
+                for kt in range(H_PASSES):
+                    nc.tensor.matmul(
+                        out=zh_ps[half][:],
+                        lhsT=hT_sb[b][:, t, kt, :],
+                        rhs=uT_sb[:, kt, halves[half]],
+                        start=(kt == 0),
+                        stop=(kt == H_PASSES - 1),
+                    )
+            zx_ps = [psum_z.tile([P, N_TILE], F32, name="zx_ps", tag="z_ps") for half in range(HALVES)]
+            for half in range(HALVES):
+                for g in range(X_PASSES):
+                    rows = slice((t * X_PASSES + g) * P, (t * X_PASSES + g + 1) * P)
+                    nc.tensor.matmul_mx(
+                        out=zx_ps[half][:],
+                        lhsT=x_codes[b][:, rows].bitcast(FP8X4),
+                        lhsT_scale=x_scales[b][:, rows],
+                        rhs=w_words[:, g, halves[half]].bitcast(FP8X4),
+                        rhs_scale=w_scales[:, g, halves[half]],
+                        start=(g == 0),
+                        stop=(g == X_PASSES - 1),
+                    )
+            for half in range(HALVES):
+                nc.vector.tensor_tensor(out=z[:, t, halves[half]], in0=zh_ps[half][:], in1=bias_sb[:, halves[half]], op=ALU.add)
+            for half in range(HALVES):
+                nc.vector.tensor_tensor(out=z[:, t, halves[half]], in0=zx_ps[half][:], in1=z[:, t, halves[half]], op=ALU.add)
 
         def gates_block(b):
             z = z_sb[b]
@@ -160,31 +171,31 @@ def tile_lstmcell_t_e_kernel(tc, x_t, h_pre, c_pre, Wx_words, Wx_scales, bW, Uh,
         def elementwise_engine(b):
             return nc.vector if b == BLOCKS - 1 else nc.gpsimd
 
-        def cell_products(b):
+        def cell_block(b):
+            rows = slice(b * BLOCK, (b + 1) * BLOCK)
             z = z_sb[b]
             fc = work.tile([P, ROW_TILES, H], F32, name="fc")
             elementwise_engine(b).tensor_tensor(out=fc[:], in0=z[:, :, 0:H], in1=c_sb[b][:], op=ALU.mult)
             ig = work.tile([P, ROW_TILES, H], F32, name="ig")
             elementwise_engine(b).tensor_tensor(out=ig[:], in0=z[:, :, H : 2 * H], in1=z[:, :, 3 * H : Z], op=ALU.mult)
-            products[b] = (fc, ig)
-
-        def cell_sum(b):
-            rows = slice(b * BLOCK, (b + 1) * BLOCK)
-            fc, ig = products[b]
             c_t = work.tile([P, ROW_TILES, H], F32, name="c_t")
             elementwise_engine(b).tensor_tensor(out=c_t[:], in0=fc[:], in1=ig[:], op=ALU.add)
             nc.sync.dma_start(out=out_1[rows, :].rearrange("(p t) n -> p t n", t=ROW_TILES), in_=c_t[:])
             c_new[b] = c_t
 
-        def hidden_block(b):
-            rows = slice(b * BLOCK, (b + 1) * BLOCK)
+        def tanh_block(b):
             tanh_c = work.tile([P, ROW_TILES, H], F32, name="tanh_c")
             nc.scalar.activation(out=tanh_c[:], in_=c_new[b][:], func=ACT.Tanh)
+            tanh_new[b] = tanh_c
+
+        def hidden_block(b):
+            rows = slice(b * BLOCK, (b + 1) * BLOCK)
             h_t = work.tile([P, ROW_TILES, H], F32, name="h_t")
-            elementwise_engine(b).tensor_tensor(out=h_t[:], in0=z_sb[b][:, :, 2 * H : 3 * H], in1=tanh_c[:], op=ALU.mult)
+            nc.vector.tensor_tensor(out=h_t[:], in0=z_sb[b][:, :, 2 * H : 3 * H], in1=tanh_new[b][:], op=ALU.mult)
             nc.sync.dma_start(out=out_0[rows, :].rearrange("(p t) n -> p t n", t=ROW_TILES), in_=h_t[:])
 
         ctx.enter_context(tc.manual_schedule())
+        sort_block(0)
         transpose_block(0)
         quantise_block(0)
 
@@ -200,16 +211,26 @@ def tile_lstmcell_t_e_kernel(tc, x_t, h_pre, c_pre, Wx_words, Wx_scales, bW, Uh,
             bias_ps = psum_z.tile([P, N_TILE], F32, name="bias_ps", tag="z_ps")
             nc.tensor.matmul(out=bias_ps[:], lhsT=ones[:], rhs=bias_rows[:, cols], start=True, stop=True)
             nc.vector.tensor_copy(out=bias_sb[:, cols], in_=bias_ps[:])
+        sort_block(1)
 
-        for step in range(1, BLOCKS + 3):
-            if step < BLOCKS:
+        def exists(b):
+            return 0 <= b < BLOCKS
+
+        for step in range(1, BLOCKS + 4):
+            if exists(step):
                 transpose_block(step)
-            if 0 <= step - 1 < BLOCKS:
-                matmul_block(step - 1)
-            if 0 <= step - 2 < BLOCKS:
+            if exists(step + 1):
+                sort_block(step + 1)
+            if exists(step - 1):
+                matmul_row_tile(step - 1, 0)
+            if exists(step):
+                quantise_block(step)
+            if exists(step - 4):
+                hidden_block(step - 4)
+            if exists(step - 1):
+                matmul_row_tile(step - 1, 1)
+            if exists(step - 2):
                 gates_block(step - 2)
-                cell_products(step - 2)
-            if 0 <= step - 3 < BLOCKS:
-                hidden_block(step - 3)
-            if 0 <= step - 2 < BLOCKS:
-                cell_sum(step - 2)
+                cell_block(step - 2)
+            if exists(step - 3):
+                tanh_block(step - 3)

@@ -129,7 +129,7 @@ def tile_lstmcell_t_e_kernel(tc, x_t, h_pre, c_pre, Wx_words, Wx_scales, bW, Uh,
             )
             x_codes[b], x_scales[b] = codes, scales
 
-        def matmul_row_tile(b, t):
+        def matmul_row_tile(b, t, transposes_of=None):
             if t == 0:
                 z_sb[b] = work.tile([P, ROW_TILES, Z], F32, name="z", bufs=4)
             z = z_sb[b]
@@ -144,6 +144,8 @@ def tile_lstmcell_t_e_kernel(tc, x_t, h_pre, c_pre, Wx_words, Wx_scales, bW, Uh,
                         start=(kt == 0),
                         stop=(kt == H_PASSES - 1),
                     )
+                if half == 0 and transposes_of is not None:
+                    transpose_block(transposes_of)
             zx_ps = [psum_z.tile([P, N_TILE], F32, name="zx_ps", tag="z_ps") for half in range(HALVES)]
             for half in range(HALVES):
                 for g in range(X_PASSES):
@@ -217,12 +219,10 @@ def tile_lstmcell_t_e_kernel(tc, x_t, h_pre, c_pre, Wx_words, Wx_scales, bW, Uh,
             return 0 <= b < BLOCKS
 
         for step in range(1, BLOCKS + 4):
-            if exists(step):
-                transpose_block(step)
+            if exists(step - 1):
+                matmul_row_tile(step - 1, 0, transposes_of=step if exists(step) else None)
             if exists(step + 1):
                 sort_block(step + 1)
-            if exists(step - 1):
-                matmul_row_tile(step - 1, 0)
             if exists(step):
                 quantise_block(step)
             if exists(step - 4):

@@ -54,6 +54,10 @@ def tile_lstmcell_t_e_kernel(tc, x_t, h_pre, c_pre, Wx_words, Wx_scales, bW, Uh,
             nc.sync.dma_start(out=c_blk[:], in_=c_pre[rows, :].rearrange("(p t) d -> p t d", t=ROW_TILES))
             c_sb.append(c_blk)
 
+        warm = const.tile([P, 1], F32)
+        nc.vector.memset(warm[:], 0.0)
+        nc.scalar.activation(out=warm[:], in_=warm[:], func=ACT.Sigmoid)
+
         w_scales = const.tile([P, X_PASSES, Z], U8, align_bytes=64)
         nc.vector.memset(w_scales[:].rearrange("p c n -> p (c n)").bitcast(I32), 0)
         bias_rows = const.tile([P, Z], BF16)
@@ -92,7 +96,8 @@ def tile_lstmcell_t_e_kernel(tc, x_t, h_pre, c_pre, Wx_words, Wx_scales, bW, Uh,
         load_c(BLOCKS - 2)
         load_c(BLOCKS - 1)
 
-        x_sorted, x_grouped, x_codes, x_scales, hT_sb, z_sb, c_new, tanh_new = {}, {}, {}, {}, {}, {}, {}, {}
+        x_sorted, x_grouped, x_codes, x_scales, hT_sb, z_sb = {}, {}, {}, {}, {}, {}
+        fc_sb, ig_sb, c_new, tanh_new, h_new = {}, {}, {}, {}, {}
 
         def sort_block(b):
             in_order = work.tile([P, ROW_TILES, X_PASSES, 2, P], F32, name="in_order")
@@ -164,49 +169,54 @@ def tile_lstmcell_t_e_kernel(tc, x_t, h_pre, c_pre, Wx_words, Wx_scales, bW, Uh,
             for half in range(HALVES):
                 nc.vector.tensor_tensor(out=z[:, t, halves[half]], in0=zx_ps[half][:], in1=z[:, t, halves[half]], op=ALU.add)
 
-        def gates_block(b):
+        def gates_row_tile(b, t, bank_by_bank=False):
             z = z_sb[b]
-            for t in range(ROW_TILES):
+            if bank_by_bank:
+                nc.scalar.activation(out=z[:, t, 0 : 2 * H], in_=z[:, t, 0 : 2 * H], func=ACT.Sigmoid)
+                nc.scalar.activation(out=z[:, t, 3 * H : Z], in_=z[:, t, 3 * H : Z], func=ACT.Tanh)
+                nc.scalar.activation(out=z[:, t, 2 * H : 3 * H], in_=z[:, t, 2 * H : 3 * H], func=ACT.Sigmoid)
+            else:
                 nc.scalar.activation(out=z[:, t, 0 : 3 * H], in_=z[:, t, 0 : 3 * H], func=ACT.Sigmoid)
                 nc.scalar.activation(out=z[:, t, 3 * H : Z], in_=z[:, t, 3 * H : Z], func=ACT.Tanh)
 
-        def elementwise_engine(b):
-            return nc.vector if b == BLOCKS - 1 else nc.gpsimd
+        def block_tile(kept, b, name, bufs=3):
+            if b not in kept:
+                kept[b] = work.tile([P, ROW_TILES, H], F32, name=name, bufs=bufs)
+            return kept[b]
 
-        def cell_block(b):
-            rows = slice(b * BLOCK, (b + 1) * BLOCK)
+        def out_rows(out, b, tiles):
+            return out[b * BLOCK : (b + 1) * BLOCK, :].rearrange("(p t) n -> p t n", t=ROW_TILES)[:, tiles, :]
+
+        def cell(b, tiles, engine):
             z = z_sb[b]
-            fc = work.tile([P, ROW_TILES, H], F32, name="fc")
-            elementwise_engine(b).tensor_tensor(out=fc[:], in0=z[:, :, 0:H], in1=c_sb[b][:], op=ALU.mult)
-            ig = work.tile([P, ROW_TILES, H], F32, name="ig")
-            elementwise_engine(b).tensor_tensor(out=ig[:], in0=z[:, :, H : 2 * H], in1=z[:, :, 3 * H : Z], op=ALU.mult)
-            c_t = work.tile([P, ROW_TILES, H], F32, name="c_t")
-            elementwise_engine(b).tensor_tensor(out=c_t[:], in0=fc[:], in1=ig[:], op=ALU.add)
-            nc.sync.dma_start(out=out_1[rows, :].rearrange("(p t) n -> p t n", t=ROW_TILES), in_=c_t[:])
-            c_new[b] = c_t
+            fc = block_tile(fc_sb, b, "fc")
+            engine.tensor_tensor(out=fc[:, tiles], in0=z[:, tiles, 0:H], in1=c_sb[b][:, tiles], op=ALU.mult)
+            ig = block_tile(ig_sb, b, "ig")
+            engine.tensor_tensor(out=ig[:, tiles], in0=z[:, tiles, H : 2 * H], in1=z[:, tiles, 3 * H : Z], op=ALU.mult)
+            c_t = block_tile(c_new, b, "c_t")
+            engine.tensor_tensor(out=c_t[:, tiles], in0=fc[:, tiles], in1=ig[:, tiles], op=ALU.add)
+            nc.sync.dma_start(out=out_rows(out_1, b, tiles), in_=c_t[:, tiles])
 
-        def tanh_block(b):
-            tanh_c = work.tile([P, ROW_TILES, H], F32, name="tanh_c")
-            nc.scalar.activation(out=tanh_c[:], in_=c_new[b][:], func=ACT.Tanh)
-            tanh_new[b] = tanh_c
+        def tanh_cell(b, tiles):
+            tanh_c = block_tile(tanh_new, b, "tanh_c", bufs=4)
+            nc.scalar.activation(out=tanh_c[:, tiles], in_=c_new[b][:, tiles], func=ACT.Tanh)
 
-        def hidden_block(b):
-            rows = slice(b * BLOCK, (b + 1) * BLOCK)
-            h_t = work.tile([P, ROW_TILES, H], F32, name="h_t")
-            nc.vector.tensor_tensor(out=h_t[:], in0=z_sb[b][:, :, 2 * H : 3 * H], in1=tanh_new[b][:], op=ALU.mult)
-            nc.sync.dma_start(out=out_0[rows, :].rearrange("(p t) n -> p t n", t=ROW_TILES), in_=h_t[:])
+        def hidden(b, tiles, engine):
+            h_t = block_tile(h_new, b, "h_t")
+            engine.tensor_tensor(out=h_t[:, tiles], in0=z_sb[b][:, tiles, 2 * H : 3 * H], in1=tanh_new[b][:, tiles], op=ALU.mult)
+            nc.sync.dma_start(out=out_rows(out_0, b, tiles), in_=h_t[:, tiles])
 
         ctx.enter_context(tc.manual_schedule())
         sort_block(0)
         transpose_block(0)
-        quantise_block(0)
 
         uT_sb = const.tile([P, H_PASSES, Z], BF16)
         for kt in range(H_PASSES):
             uT_ps = psum_z.tile([P, Z], BF16, name="uT_ps", tag="z_ps")
             for a in range(Z // P):
                 nc.tensor.transpose(uT_ps[:, a * P : (a + 1) * P], uh_sb[:, a, kt * P : (kt + 1) * P], ident_bf16[:])
-            nc.scalar.copy(out=uT_sb[:, kt, :], in_=uT_ps[:])
+            nc.vector.tensor_copy(out=uT_sb[:, kt, :], in_=uT_ps[:])
+        quantise_block(0)
         bias_sb = const.tile([P, Z], F32)
         for half in range(HALVES):
             cols = slice(half * N_TILE, (half + 1) * N_TILE)
@@ -218,19 +228,39 @@ def tile_lstmcell_t_e_kernel(tc, x_t, h_pre, c_pre, Wx_words, Wx_scales, bW, Uh,
         def exists(b):
             return 0 <= b < BLOCKS
 
-        for step in range(1, BLOCKS + 4):
-            if exists(step - 1):
-                matmul_row_tile(step - 1, 0, transposes_of=step if exists(step) else None)
+        whole = slice(0, ROW_TILES)
+        first, second = slice(0, 1), slice(1, 2)
+        for step in range(1, BLOCKS):
+            matmul_row_tile(step - 1, 0, transposes_of=step)
             if exists(step + 1):
                 sort_block(step + 1)
-            if exists(step):
-                quantise_block(step)
+            quantise_block(step)
             if exists(step - 4):
-                hidden_block(step - 4)
-            if exists(step - 1):
-                matmul_row_tile(step - 1, 1)
+                hidden(step - 4, whole, nc.vector)
+            matmul_row_tile(step - 1, 1)
             if exists(step - 2):
-                gates_block(step - 2)
-                cell_block(step - 2)
+                gates_row_tile(step - 2, 0)
+                gates_row_tile(step - 2, 1)
+                cell(step - 2, whole, nc.gpsimd)
             if exists(step - 3):
-                tanh_block(step - 3)
+                tanh_cell(step - 3, whole)
+
+        last = BLOCKS - 1
+        matmul_row_tile(last, 0)
+        hidden(last - 3, whole, nc.gpsimd)
+        matmul_row_tile(last, 1)
+        gates_row_tile(last - 1, 0)
+        cell(last - 1, first, nc.gpsimd)
+        gates_row_tile(last - 1, 1)
+        tanh_cell(last - 2, whole)
+        gates_row_tile(last, 0)
+        cell(last - 1, second, nc.vector)
+        cell(last, first, nc.vector)
+        gates_row_tile(last, 1, bank_by_bank=True)
+        tanh_cell(last - 1, whole)
+        hidden(last - 2, whole, nc.vector)
+        cell(last, second, nc.vector)
+        tanh_cell(last, first)
+        hidden(last - 1, whole, nc.vector)
+        tanh_cell(last, second)
+        hidden(last, whole, nc.vector)

@@ -66,8 +66,6 @@ def tile_lstmcell_t_e_kernel(tc, x_t, h_pre, c_pre, Wx_words, Wx_scales, bW, Uh,
         nc.vector.memset(ones[:], 1.0)
         ident_f32 = const.tile([P, P], F32)
         make_identity(nc, ident_f32[:])
-        ident_bf16 = const.tile([P, P], BF16)
-        make_identity(nc, ident_bf16[:])
 
         load_x_h(0)
         uh_sb = const.tile([P, Z // P, H], BF16)
@@ -116,12 +114,11 @@ def tile_lstmcell_t_e_kernel(tc, x_t, h_pre, c_pre, Wx_words, Wx_scales, bW, Uh,
                     for u in range(2):
                         nc.tensor.transpose(xT_ps[:, g, u, :], x_sorted[b][:, t, g, u, :], ident_f32[:])
                 nc.scalar.copy(out=grouped[:, t].bitcast(F32), in_=xT_ps[:].rearrange("p g u r -> p g r u"))
-            hT_ps = psum_t.tile([P, ROW_TILES, H_PASSES, P], BF16, name="hT_ps")
+            hT_ps = psum_t.tile([P, ROW_TILES, P], F32, name="hT_ps")
             for t in range(ROW_TILES):
-                for kt in range(H_PASSES):
-                    nc.tensor.transpose(hT_ps[:, t, kt, :], h_sb[b][:, t, kt * P : (kt + 1) * P], ident_bf16[:])
+                nc.tensor.transpose(hT_ps[:, t, :], h_sb[b][:, t, :].bitcast(F32), ident_f32[:])
             hT = work.tile([P, ROW_TILES, H_PASSES, P], BF16, name="hT")
-            nc.scalar.copy(out=hT[:], in_=hT_ps[:])
+            nc.scalar.copy(out=hT[:], in_=hT_ps[:].bitcast(BF16).rearrange("p t (r e) -> p t e r", e=H_PASSES))
             x_grouped[b], hT_sb[b] = grouped, hT
 
         def quantise_block(b):
@@ -211,11 +208,14 @@ def tile_lstmcell_t_e_kernel(tc, x_t, h_pre, c_pre, Wx_words, Wx_scales, bW, Uh,
         transpose_block(0)
 
         uT_sb = const.tile([P, H_PASSES, Z], BF16)
-        for kt in range(H_PASSES):
-            uT_ps = psum_z.tile([P, Z], BF16, name="uT_ps", tag="z_ps")
-            for a in range(Z // P):
-                nc.tensor.transpose(uT_ps[:, a * P : (a + 1) * P], uh_sb[:, a, kt * P : (kt + 1) * P], ident_bf16[:])
-            nc.vector.tensor_copy(out=uT_sb[:, kt, :], in_=uT_ps[:])
+        for half in range(HALVES):
+            uT_ps = psum_z.tile([P, N_TILE], F32, name="uT_ps", tag="z_ps")
+            for a in range(N_TILE // P):
+                nc.tensor.transpose(uT_ps[:, a * P : (a + 1) * P], uh_sb[:, half * (N_TILE // P) + a, :].bitcast(F32), ident_f32[:])
+            nc.vector.tensor_copy(
+                out=uT_sb[:, :, half * N_TILE : (half + 1) * N_TILE],
+                in_=uT_ps[:].bitcast(BF16).rearrange("p (n e) -> p e n", e=H_PASSES),
+            )
         quantise_block(0)
         bias_sb = const.tile([P, Z], F32)
         for half in range(HALVES):

@@ -110,9 +110,13 @@ def tile_lstmcell_t_e_kernel(tc, x_t, h_pre, c_pre, Wx_words, Wx_scales, bW, Uh,
             grouped = work.tile([P, ROW_TILES, X_PASSES, P, PACK], BF16, align_bytes=64, name="grouped")
             for t in range(ROW_TILES):
                 xT_ps = psum_t.tile([P, X_PASSES, 2, P], F32, name="xT_ps%d" % t)
+                if b in x_sorted:
+                    words = x_sorted[b][:, t]
+                else:
+                    words = x_sb[b][:, t, :].bitcast(F32).rearrange("p (g j u) -> p g u j", g=X_PASSES, u=2)
                 for g in range(X_PASSES):
                     for u in range(2):
-                        nc.tensor.transpose(xT_ps[:, g, u, :], x_sorted[b][:, t, g, u, :], ident_f32[:])
+                        nc.tensor.transpose(xT_ps[:, g, u, :], words[:, g, u, :], ident_f32[:])
                 nc.scalar.copy(out=grouped[:, t].bitcast(F32), in_=xT_ps[:].rearrange("p g u r -> p g r u"))
             hT_ps = psum_t.tile([P, ROW_TILES, P], F32, name="hT_ps")
             for t in range(ROW_TILES):
@@ -131,11 +135,12 @@ def tile_lstmcell_t_e_kernel(tc, x_t, h_pre, c_pre, Wx_words, Wx_scales, bW, Uh,
             )
             x_codes[b], x_scales[b] = codes, scales
 
-        def matmul_row_tile(b, t, transposes_of=None):
+        halves = [slice(half * N_TILE, (half + 1) * N_TILE) for half in range(HALVES)]
+
+        def plain_row_tile(b, t, transposes_of=None):
             if t == 0:
                 z_sb[b] = work.tile([P, ROW_TILES, Z], F32, name="z", bufs=4)
             z = z_sb[b]
-            halves = [slice(half * N_TILE, (half + 1) * N_TILE) for half in range(HALVES)]
             zh_ps = [psum_z.tile([P, N_TILE], F32, name="zh_ps", tag="z_ps") for half in range(HALVES)]
             for half in range(HALVES):
                 for kt in range(H_PASSES):
@@ -148,6 +153,11 @@ def tile_lstmcell_t_e_kernel(tc, x_t, h_pre, c_pre, Wx_words, Wx_scales, bW, Uh,
                     )
                 if half == 0 and transposes_of is not None:
                     transpose_block(transposes_of)
+            for half in range(HALVES):
+                nc.vector.tensor_tensor(out=z[:, t, halves[half]], in0=zh_ps[half][:], in1=bias_sb[:, halves[half]], op=ALU.add)
+
+        def mx_row_tile(b, t):
+            z = z_sb[b]
             zx_ps = [psum_z.tile([P, N_TILE], F32, name="zx_ps", tag="z_ps") for half in range(HALVES)]
             for half in range(HALVES):
                 for g in range(X_PASSES):
@@ -162,9 +172,11 @@ def tile_lstmcell_t_e_kernel(tc, x_t, h_pre, c_pre, Wx_words, Wx_scales, bW, Uh,
                         stop=(g == X_PASSES - 1),
                     )
             for half in range(HALVES):
-                nc.vector.tensor_tensor(out=z[:, t, halves[half]], in0=zh_ps[half][:], in1=bias_sb[:, halves[half]], op=ALU.add)
-            for half in range(HALVES):
                 nc.vector.tensor_tensor(out=z[:, t, halves[half]], in0=zx_ps[half][:], in1=z[:, t, halves[half]], op=ALU.add)
+
+        def matmul_row_tile(b, t, transposes_of=None):
+            plain_row_tile(b, t, transposes_of)
+            mx_row_tile(b, t)
 
         def gates_row_tile(b, t, bank_by_bank=False):
             z = z_sb[b]
@@ -204,26 +216,22 @@ def tile_lstmcell_t_e_kernel(tc, x_t, h_pre, c_pre, Wx_words, Wx_scales, bW, Uh,
             nc.sync.dma_start(out=out_rows(out_0, b, tiles), in_=h_t[:, tiles])
 
         ctx.enter_context(tc.manual_schedule())
-        sort_block(0)
         transpose_block(0)
-
+        bias_sb = const.tile([P, Z], F32)
+        for half in range(HALVES):
+            bias_ps = psum_z.tile([P, N_TILE], F32, name="bias_ps", tag="z_ps")
+            nc.tensor.matmul(out=bias_ps[:], lhsT=ones[:], rhs=bias_rows[:, halves[half]], start=True, stop=True)
+            nc.scalar.copy(out=bias_sb[:, halves[half]], in_=bias_ps[:])
         uT_sb = const.tile([P, H_PASSES, Z], BF16)
         for half in range(HALVES):
             uT_ps = psum_z.tile([P, N_TILE], F32, name="uT_ps", tag="z_ps")
             for a in range(N_TILE // P):
                 nc.tensor.transpose(uT_ps[:, a * P : (a + 1) * P], uh_sb[:, half * (N_TILE // P) + a, :].bitcast(F32), ident_f32[:])
             nc.vector.tensor_copy(
-                out=uT_sb[:, :, half * N_TILE : (half + 1) * N_TILE],
+                out=uT_sb[:, :, halves[half]],
                 in_=uT_ps[:].bitcast(BF16).rearrange("p (n e) -> p e n", e=H_PASSES),
             )
         quantise_block(0)
-        bias_sb = const.tile([P, Z], F32)
-        for half in range(HALVES):
-            cols = slice(half * N_TILE, (half + 1) * N_TILE)
-            bias_ps = psum_z.tile([P, N_TILE], F32, name="bias_ps", tag="z_ps")
-            nc.tensor.matmul(out=bias_ps[:], lhsT=ones[:], rhs=bias_rows[:, cols], start=True, stop=True)
-            nc.vector.tensor_copy(out=bias_sb[:, cols], in_=bias_ps[:])
-        sort_block(1)
 
         def exists(b):
             return 0 <= b < BLOCKS
@@ -231,13 +239,21 @@ def tile_lstmcell_t_e_kernel(tc, x_t, h_pre, c_pre, Wx_words, Wx_scales, bW, Uh,
         whole = slice(0, ROW_TILES)
         first, second = slice(0, 1), slice(1, 2)
         for step in range(1, BLOCKS):
-            matmul_row_tile(step - 1, 0, transposes_of=step)
+            if step == 1:
+                plain_row_tile(0, 0, transposes_of=1)
+                plain_row_tile(0, 1)
+                mx_row_tile(0, 0)
+            else:
+                matmul_row_tile(step - 1, 0, transposes_of=step)
             if exists(step + 1):
                 sort_block(step + 1)
             quantise_block(step)
             if exists(step - 4):
                 hidden(step - 4, whole, nc.vector)
-            matmul_row_tile(step - 1, 1)
+            if step == 1:
+                mx_row_tile(0, 1)
+            else:
+                matmul_row_tile(step - 1, 1)
             if exists(step - 2):
                 gates_row_tile(step - 2, 0)
                 gates_row_tile(step - 2, 1)

@@ -39,13 +39,14 @@ def tile_lstmcell_t_e_kernel(tc, x_t, h_pre, c_pre, Wx_words, Wx_scales, bW, Uh,
 
         x_sb, h_sb, c_sb = [], [], []
 
-        def load_x_h(b):
-            rows = slice(b * BLOCK, (b + 1) * BLOCK)
+        def load_x(b):
             x_blk = inputs.tile([P, ROW_TILES, D], BF16, name="x_blk")
-            nc.sync.dma_start(out=x_blk[:], in_=x_t[rows, :].rearrange("(p t) d -> p t d", t=ROW_TILES))
-            h_blk = inputs.tile([P, ROW_TILES, H], BF16, name="h_blk")
-            nc.sync.dma_start(out=h_blk[:], in_=h_pre[rows, :].rearrange("(p t) d -> p t d", t=ROW_TILES))
+            nc.sync.dma_start(out=x_blk[:], in_=x_t[b * BLOCK : (b + 1) * BLOCK, :].rearrange("(p t) d -> p t d", t=ROW_TILES))
             x_sb.append(x_blk)
+
+        def load_h(b):
+            h_blk = inputs.tile([P, ROW_TILES, H], BF16, name="h_blk")
+            nc.sync.dma_start(out=h_blk[:], in_=h_pre[b * BLOCK : (b + 1) * BLOCK, :].rearrange("(p t) d -> p t d", t=ROW_TILES))
             h_sb.append(h_blk)
 
         def load_c(b):
@@ -67,29 +68,32 @@ def tile_lstmcell_t_e_kernel(tc, x_t, h_pre, c_pre, Wx_words, Wx_scales, bW, Uh,
         ident_f32 = const.tile([P, P], F32)
         make_identity(nc, ident_f32[:])
 
-        load_x_h(0)
+        load_h(0)
         uh_sb = const.tile([P, Z // P, H], BF16)
         nc.sync.dma_start(out=uh_sb[:], in_=Uh.rearrange("e (a p) k -> p (e a) k", p=P))
         nc.sync.dma_start(out=bias_rows[0:1, :], in_=bW.rearrange("(o e) n -> o (e n)", o=1))
         nc.sync.dma_start(out=bias_rows[1:2, :], in_=bU.rearrange("(o e) n -> o (e n)", o=1))
-        load_x_h(1)
-
+        load_x(0)
+        w_words = const.tile([P, X_PASSES, Z], U32, align_bytes=64)
         scale_words = Wx_scales.bitcast(I32).rearrange("(e c) q n -> c q e n", c=X_PASSES)
+        code_words = Wx_words.rearrange("g p n t -> g p (n t)").bitcast(I32).rearrange("(e c) p n -> c p e n", c=X_PASSES)
         for c in range(X_PASSES):
             for quad in range(4):
                 nc.sync.dma_start(
                     out=w_scales[32 * quad : 32 * quad + 4, c, :].bitcast(I32).rearrange("q (e n) -> q e n", e=GATES),
                     in_=scale_words[c, 4 * quad : 4 * quad + 4],
                 )
-        w_words = const.tile([P, X_PASSES, Z], U32, align_bytes=64)
-        code_words = Wx_words.rearrange("g p n t -> g p (n t)").bitcast(I32).rearrange("(e c) p n -> c p e n", c=X_PASSES)
+            if c == 0:
+                load_x(1)
+                load_h(1)
         for c in range(X_PASSES):
             nc.sync.dma_start(
                 out=w_words[:, c, :].bitcast(I32).rearrange("p (e n) -> p e n", e=GATES),
                 in_=code_words[c],
             )
         for b in range(2, BLOCKS):
-            load_x_h(b)
+            load_x(b)
+            load_h(b)
             load_c(b - 2)
         load_c(BLOCKS - 2)
         load_c(BLOCKS - 1)
@@ -106,7 +110,7 @@ def tile_lstmcell_t_e_kernel(tc, x_t, h_pre, c_pre, Wx_words, Wx_scales, bW, Uh,
                 )
             x_sorted[b] = in_order
 
-        def transpose_block(b):
+        def transpose_x(b, copies):
             grouped = work.tile([P, ROW_TILES, X_PASSES, P, PACK], BF16, align_bytes=64, name="grouped")
             for t in range(ROW_TILES):
                 xT_ps = psum_t.tile([P, X_PASSES, 2, P], F32, name="xT_ps%d" % t)
@@ -117,13 +121,20 @@ def tile_lstmcell_t_e_kernel(tc, x_t, h_pre, c_pre, Wx_words, Wx_scales, bW, Uh,
                 for g in range(X_PASSES):
                     for u in range(2):
                         nc.tensor.transpose(xT_ps[:, g, u, :], words[:, g, u, :], ident_f32[:])
-                nc.scalar.copy(out=grouped[:, t].bitcast(F32), in_=xT_ps[:].rearrange("p g u r -> p g r u"))
+                copies[t](out=grouped[:, t].bitcast(F32), in_=xT_ps[:].rearrange("p g u r -> p g r u"))
+            x_grouped[b] = grouped
+
+        def transpose_h(b):
             hT_ps = psum_t.tile([P, ROW_TILES, P], F32, name="hT_ps")
             for t in range(ROW_TILES):
                 nc.tensor.transpose(hT_ps[:, t, :], h_sb[b][:, t, :].bitcast(F32), ident_f32[:])
-            hT = work.tile([P, ROW_TILES, H_PASSES, P], BF16, name="hT")
-            nc.scalar.copy(out=hT[:], in_=hT_ps[:].bitcast(BF16).rearrange("p t (r e) -> p t e r", e=H_PASSES))
-            x_grouped[b], hT_sb[b] = grouped, hT
+            hT = work.tile([P, ROW_TILES, P], F32, name="hT")
+            nc.scalar.copy(out=hT[:], in_=hT_ps[:])
+            hT_sb[b] = hT
+
+        def transpose_block(b):
+            transpose_x(b, [nc.scalar.copy, nc.scalar.copy])
+            transpose_h(b)
 
         def quantise_block(b):
             codes = work.tile([P, ROW_TILES * X_PASSES * P], U32, align_bytes=64, name="codes")
@@ -146,8 +157,8 @@ def tile_lstmcell_t_e_kernel(tc, x_t, h_pre, c_pre, Wx_words, Wx_scales, bW, Uh,
                 for kt in range(H_PASSES):
                     nc.tensor.matmul(
                         out=zh_ps[half][:],
-                        lhsT=hT_sb[b][:, t, kt, :],
-                        rhs=uT_sb[:, kt, halves[half]],
+                        lhsT=hT_sb[b][:, t, :].bitcast(BF16).rearrange("p (r e) -> p e r", e=H_PASSES)[:, kt, :],
+                        rhs=uT_sb[:, 2 * half : 2 * half + 2, kt, :],
                         start=(kt == 0),
                         stop=(kt == H_PASSES - 1),
                     )
@@ -216,21 +227,22 @@ def tile_lstmcell_t_e_kernel(tc, x_t, h_pre, c_pre, Wx_words, Wx_scales, bW, Uh,
             nc.sync.dma_start(out=out_rows(out_0, b, tiles), in_=h_t[:, tiles])
 
         ctx.enter_context(tc.manual_schedule())
-        transpose_block(0)
+        transpose_h(0)
+        uT_sb = const.tile([P, GATES, H_PASSES, H], BF16)
+        for gate in range(GATES):
+            uT_ps = psum_z.tile([P, H], F32, name="uT_ps", tag="z_ps")
+            for a in range(H // P):
+                nc.tensor.transpose(uT_ps[:, a * P : (a + 1) * P], uh_sb[:, gate * (H // P) + a, :].bitcast(F32), ident_f32[:])
+            copy = nc.vector.tensor_copy if gate % 2 == 0 else nc.scalar.copy
+            copy(out=uT_sb[:, gate], in_=uT_ps[:].bitcast(BF16).rearrange("p (n e) -> p e n", e=H_PASSES))
         bias_sb = const.tile([P, Z], F32)
+        bias_ps = [psum_z.tile([P, N_TILE], F32, name="bias_ps", tag="z_ps") for half in range(HALVES)]
         for half in range(HALVES):
-            bias_ps = psum_z.tile([P, N_TILE], F32, name="bias_ps", tag="z_ps")
-            nc.tensor.matmul(out=bias_ps[:], lhsT=ones[:], rhs=bias_rows[:, halves[half]], start=True, stop=True)
-            nc.scalar.copy(out=bias_sb[:, halves[half]], in_=bias_ps[:])
-        uT_sb = const.tile([P, H_PASSES, Z], BF16)
+            nc.tensor.matmul(out=bias_ps[half][:], lhsT=ones[:], rhs=bias_rows[:, halves[half]], start=True, stop=True)
+        transpose_x(0, [nc.scalar.copy, nc.vector.tensor_copy])
         for half in range(HALVES):
-            uT_ps = psum_z.tile([P, N_TILE], F32, name="uT_ps", tag="z_ps")
-            for a in range(N_TILE // P):
-                nc.tensor.transpose(uT_ps[:, a * P : (a + 1) * P], uh_sb[:, half * (N_TILE // P) + a, :].bitcast(F32), ident_f32[:])
-            nc.vector.tensor_copy(
-                out=uT_sb[:, :, halves[half]],
-                in_=uT_ps[:].bitcast(BF16).rearrange("p (n e) -> p e n", e=H_PASSES),
-            )
+            nc.scalar.copy(out=bias_sb[:, halves[half]], in_=bias_ps[half][:])
+        sort_block(1)
         quantise_block(0)
 
         def exists(b):
@@ -240,8 +252,9 @@ def tile_lstmcell_t_e_kernel(tc, x_t, h_pre, c_pre, Wx_words, Wx_scales, bW, Uh,
         first, second = slice(0, 1), slice(1, 2)
         for step in range(1, BLOCKS):
             if step == 1:
-                plain_row_tile(0, 0, transposes_of=1)
+                plain_row_tile(0, 0)
                 plain_row_tile(0, 1)
+                transpose_block(1)
                 mx_row_tile(0, 0)
             else:
                 matmul_row_tile(step - 1, 0, transposes_of=step)

@@ -148,7 +148,7 @@ def tile_lstmcell_t_e_kernel(tc, x_t, h_pre, c_pre, Wx_words, Wx_scales, bW, Uh,
 
         halves = [slice(half * N_TILE, (half + 1) * N_TILE) for half in range(HALVES)]
 
-        def plain_row_tile(b, t, transposes_of=None):
+        def plain_row_tile(b, t, transposes_of=None, between=None):
             if t == 0:
                 z_sb[b] = work.tile([P, ROW_TILES, Z], F32, name="z", bufs=4)
             z = z_sb[b]
@@ -166,6 +166,8 @@ def tile_lstmcell_t_e_kernel(tc, x_t, h_pre, c_pre, Wx_words, Wx_scales, bW, Uh,
                     transpose_block(transposes_of)
             for half in range(HALVES):
                 nc.vector.tensor_tensor(out=z[:, t, halves[half]], in0=zh_ps[half][:], in1=bias_sb[:, halves[half]], op=ALU.add)
+                if half == 0 and between is not None:
+                    between()
 
         def mx_row_tile(b, t):
             z = z_sb[b]
@@ -207,15 +209,21 @@ def tile_lstmcell_t_e_kernel(tc, x_t, h_pre, c_pre, Wx_words, Wx_scales, bW, Uh,
         def out_rows(out, b, tiles):
             return out[b * BLOCK : (b + 1) * BLOCK, :].rearrange("(p t) n -> p t n", t=ROW_TILES)[:, tiles, :]
 
-        def cell(b, tiles, engine):
+        def cell_products(b, tiles, engine):
             z = z_sb[b]
             fc = block_tile(fc_sb, b, "fc")
             engine.tensor_tensor(out=fc[:, tiles], in0=z[:, tiles, 0:H], in1=c_sb[b][:, tiles], op=ALU.mult)
             ig = block_tile(ig_sb, b, "ig")
             engine.tensor_tensor(out=ig[:, tiles], in0=z[:, tiles, H : 2 * H], in1=z[:, tiles, 3 * H : Z], op=ALU.mult)
+
+        def cell_sum(b, tiles, engine):
             c_t = block_tile(c_new, b, "c_t")
-            engine.tensor_tensor(out=c_t[:, tiles], in0=fc[:, tiles], in1=ig[:, tiles], op=ALU.add)
+            engine.tensor_tensor(out=c_t[:, tiles], in0=fc_sb[b][:, tiles], in1=ig_sb[b][:, tiles], op=ALU.add)
             nc.sync.dma_start(out=out_rows(out_1, b, tiles), in_=c_t[:, tiles])
+
+        def cell(b, tiles, engine):
+            cell_products(b, tiles, engine)
+            cell_sum(b, tiles, engine)
 
         def tanh_cell(b, tiles):
             tanh_c = block_tile(tanh_new, b, "tanh_c", bufs=4)
@@ -250,46 +258,56 @@ def tile_lstmcell_t_e_kernel(tc, x_t, h_pre, c_pre, Wx_words, Wx_scales, bW, Uh,
 
         whole = slice(0, ROW_TILES)
         first, second = slice(0, 1), slice(1, 2)
+
+        def shared_port_work(b, step):
+            if exists(b):
+                hidden(b, whole, nc.vector)
+            quantise_block(step)
+
         for step in range(1, BLOCKS):
+            a = step - 1
             if step == 1:
                 plain_row_tile(0, 0)
                 plain_row_tile(0, 1)
                 transpose_block(1)
-                mx_row_tile(0, 0)
             else:
-                matmul_row_tile(step - 1, 0, transposes_of=step)
+                plain_row_tile(a, 0, step, lambda: shared_port_work(a - 3, step))
+            if exists(a - 1):
+                gates_row_tile(a - 1, 1)
+                cell(a - 1, whole, nc.gpsimd)
+            mx_row_tile(a, 0)
             if exists(step + 1):
                 sort_block(step + 1)
-            quantise_block(step)
-            if exists(step - 4):
-                hidden(step - 4, whole, nc.vector)
             if step == 1:
-                mx_row_tile(0, 1)
-            else:
-                matmul_row_tile(step - 1, 1)
-            if exists(step - 2):
-                gates_row_tile(step - 2, 0)
-                gates_row_tile(step - 2, 1)
-                cell(step - 2, whole, nc.gpsimd)
-            if exists(step - 3):
-                tanh_cell(step - 3, whole)
+                quantise_block(1)
+            if exists(a - 2):
+                tanh_cell(a - 2, whole)
+            if step > 1:
+                plain_row_tile(a, 1)
+            gates_row_tile(a, 0)
+            mx_row_tile(a, 1)
 
         last = BLOCKS - 1
-        matmul_row_tile(last, 0)
-        hidden(last - 3, whole, nc.gpsimd)
-        matmul_row_tile(last, 1)
-        gates_row_tile(last - 1, 0)
         cell(last - 1, first, nc.gpsimd)
         gates_row_tile(last - 1, 1)
+        cell_products(last - 1, second, nc.gpsimd)
+        plain_row_tile(last, 0)
         tanh_cell(last - 2, whole)
+        mx_row_tile(last, 0)
+        plain_row_tile(last, 1)
         gates_row_tile(last, 0)
-        cell(last - 1, second, nc.vector)
-        cell(last, first, nc.vector)
+        mx_row_tile(last, 1)
+        hidden(last - 3, whole, nc.vector)
+        cell_sum(last - 1, second, nc.vector)
+        cell_products(last, first, nc.vector)
+        hidden(last - 2, whole, nc.vector)
         gates_row_tile(last, 1, bank_by_bank=True)
         tanh_cell(last - 1, whole)
-        hidden(last - 2, whole, nc.vector)
-        cell(last, second, nc.vector)
+        cell_sum(last, first, nc.vector)
         tanh_cell(last, first)
+        cell_products(last, second, nc.vector)
         hidden(last - 1, whole, nc.vector)
+        cell_sum(last, second, nc.vector)
         tanh_cell(last, second)
-        hidden(last, whole, nc.vector)
+        hidden(last, first, nc.vector)
+        hidden(last, second, nc.vector)

@@ -26,6 +26,7 @@ HALVES = Z // N_TILE
 ROW_TILES = 2
 BLOCK = ROW_TILES * P
 BLOCKS = B // BLOCK
+WARM_UP = 4
 
 
 def tile_lstmcell_t_e_kernel(tc, x_t, h_pre, c_pre, Wx_words, Wx_scales, bW, Uh, bU, out_0, out_1):
@@ -59,12 +60,14 @@ def tile_lstmcell_t_e_kernel(tc, x_t, h_pre, c_pre, Wx_words, Wx_scales, bW, Uh,
         nc.vector.memset(warm[:], 0.0)
         nc.scalar.activation(out=warm[:], in_=warm[:], func=ACT.Sigmoid)
 
+        ones = const.tile([P, P], BF16)
+        nc.vector.memset(ones[:], 1.0)
+        spare = const.tile([P, N_TILE], BF16)
+        nc.vector.memset(spare[:], 0.0)
         w_scales = const.tile([P, X_PASSES, Z], U8, align_bytes=64)
         nc.vector.memset(w_scales[:].rearrange("p c n -> p (c n)").bitcast(I32), 0)
         bias_rows = const.tile([P, Z], BF16)
         nc.vector.memset(bias_rows[:], 0.0)
-        ones = const.tile([P, P], BF16)
-        nc.vector.memset(ones[:], 1.0)
         ident_f32 = const.tile([P, P], F32)
         make_identity(nc, ident_f32[:])
 
@@ -235,6 +238,10 @@ def tile_lstmcell_t_e_kernel(tc, x_t, h_pre, c_pre, Wx_words, Wx_scales, bW, Uh,
             nc.sync.dma_start(out=out_rows(out_0, b, tiles), in_=h_t[:, tiles])
 
         ctx.enter_context(tc.manual_schedule())
+
+        spare_ps = psum_t.tile([P, N_TILE], F32, name="spare_ps", tag="xT_ps1")
+        for i in range(WARM_UP):
+            nc.tensor.matmul(out=spare_ps[:], lhsT=ones[:], rhs=spare[:], start=True, stop=True)
         transpose_h(0)
         uT_sb = const.tile([P, GATES, H_PASSES, H], BF16)
         for gate in range(GATES):

@@ -26,6 +26,7 @@ HALVES = Z // N_TILE
 ROW_TILES = 2
 BLOCK = ROW_TILES * P
 BLOCKS = B // BLOCK
+AHEAD = 6
 WARM_UP = 4
 
 
@@ -37,6 +38,9 @@ def tile_lstmcell_t_e_kernel(tc, x_t, h_pre, c_pre, Wx_words, Wx_scales, bW, Uh,
         work = ctx.enter_context(tc.tile_pool(name="work", bufs=3))
         psum_t = ctx.enter_context(tc.psum_pool(name="psum_t", bufs=1))
         psum_z = ctx.enter_context(tc.psum_pool(name="psum_z", bufs=5))
+
+        def exists(b):
+            return 0 <= b < BLOCKS
 
         x_sb, h_sb, c_sb = [], [], []
 
@@ -94,12 +98,15 @@ def tile_lstmcell_t_e_kernel(tc, x_t, h_pre, c_pre, Wx_words, Wx_scales, bW, Uh,
                 out=w_words[:, c, :].bitcast(I32).rearrange("p (e n) -> p e n", e=GATES),
                 in_=code_words[c],
             )
-        for b in range(2, BLOCKS):
-            load_x(b)
-            load_h(b)
-            load_c(b - 2)
-        load_c(BLOCKS - 2)
-        load_c(BLOCKS - 1)
+        def load_block(b):
+            if exists(b):
+                load_x(b)
+                load_h(b)
+            if exists(b - 2):
+                load_c(b - 2)
+
+        for b in range(2, AHEAD):
+            load_block(b)
 
         x_sorted, x_grouped, x_codes, x_scales, hT_sb, z_sb = {}, {}, {}, {}, {}, {}
         fc_sb, ig_sb, c_new, tanh_new, h_new = {}, {}, {}, {}, {}
@@ -137,7 +144,8 @@ def tile_lstmcell_t_e_kernel(tc, x_t, h_pre, c_pre, Wx_words, Wx_scales, bW, Uh,
 
         def transpose_block(b):
             transpose_x(b, [nc.scalar.copy, nc.scalar.copy])
-            transpose_h(b)
+            if b > 0:
+                transpose_h(b)
 
         def quantise_block(b):
             codes = work.tile([P, ROW_TILES * X_PASSES * P], U32, align_bytes=64, name="codes")
@@ -161,7 +169,7 @@ def tile_lstmcell_t_e_kernel(tc, x_t, h_pre, c_pre, Wx_words, Wx_scales, bW, Uh,
                     nc.tensor.matmul(
                         out=zh_ps[half][:],
                         lhsT=hT_sb[b][:, t, :].bitcast(BF16).rearrange("p (r e) -> p e r", e=H_PASSES)[:, kt, :],
-                        rhs=uT_sb[:, 2 * half : 2 * half + 2, kt, :],
+                        rhs=uT_sb[:, half, kt, :],
                         start=(kt == 0),
                         stop=(kt == H_PASSES - 1),
                     )
@@ -243,25 +251,20 @@ def tile_lstmcell_t_e_kernel(tc, x_t, h_pre, c_pre, Wx_words, Wx_scales, bW, Uh,
         for i in range(WARM_UP):
             nc.tensor.matmul(out=spare_ps[:], lhsT=ones[:], rhs=spare[:], start=True, stop=True)
         transpose_h(0)
-        uT_sb = const.tile([P, GATES, H_PASSES, H], BF16)
+        uT_sb = const.tile([P, HALVES, H_PASSES, N_TILE], BF16)
         for gate in range(GATES):
             uT_ps = psum_z.tile([P, H], F32, name="uT_ps", tag="z_ps")
             for a in range(H // P):
                 nc.tensor.transpose(uT_ps[:, a * P : (a + 1) * P], uh_sb[:, gate * (H // P) + a, :].bitcast(F32), ident_f32[:])
             copy = nc.vector.tensor_copy if gate % 2 == 0 else nc.scalar.copy
-            copy(out=uT_sb[:, gate], in_=uT_ps[:].bitcast(BF16).rearrange("p (n e) -> p e n", e=H_PASSES))
+            half, place = divmod(gate, GATES // HALVES)
+            copy(out=uT_sb[:, half, :, place * H : (place + 1) * H], in_=uT_ps[:].bitcast(BF16).rearrange("p (n e) -> p e n", e=H_PASSES))
         bias_sb = const.tile([P, Z], F32)
-        bias_ps = [psum_z.tile([P, N_TILE], F32, name="bias_ps", tag="z_ps") for half in range(HALVES)]
+        bias_ps = [psum_t.tile([P, N_TILE], F32, name="bias_ps0", tag="hT_ps"), psum_z.tile([P, N_TILE], F32, name="bias_ps1", tag="z_ps")]
         for half in range(HALVES):
             nc.tensor.matmul(out=bias_ps[half][:], lhsT=ones[:], rhs=bias_rows[:, halves[half]], start=True, stop=True)
-        transpose_x(0, [nc.scalar.copy, nc.vector.tensor_copy])
         for half in range(HALVES):
             nc.scalar.copy(out=bias_sb[:, halves[half]], in_=bias_ps[half][:])
-        sort_block(1)
-        quantise_block(0)
-
-        def exists(b):
-            return 0 <= b < BLOCKS
 
         whole = slice(0, ROW_TILES)
         first, second = slice(0, 1), slice(1, 2)
@@ -273,9 +276,12 @@ def tile_lstmcell_t_e_kernel(tc, x_t, h_pre, c_pre, Wx_words, Wx_scales, bW, Uh,
 
         for step in range(1, BLOCKS):
             a = step - 1
+            load_block(a + AHEAD)
             if step == 1:
-                plain_row_tile(0, 0)
+                plain_row_tile(0, 0, 0)
+                quantise_block(0)
                 plain_row_tile(0, 1)
+                sort_block(1)
                 transpose_block(1)
             else:
                 plain_row_tile(a, 0, step, lambda: shared_port_work(a - 3, step))

@@ -26,8 +26,8 @@ HALVES = Z // N_TILE
 ROW_TILES = 2
 BLOCK = ROW_TILES * P
 BLOCKS = B // BLOCK
-AHEAD = 6
-WARM_UP = 4
+AHEAD = 4
+WARM_UP = 3
 
 
 def tile_lstmcell_t_e_kernel(tc, x_t, h_pre, c_pre, Wx_words, Wx_scales, bW, Uh, bU, out_0, out_1):
@@ -60,6 +60,9 @@ def tile_lstmcell_t_e_kernel(tc, x_t, h_pre, c_pre, Wx_words, Wx_scales, bW, Uh,
             nc.sync.dma_start(out=c_blk[:], in_=c_pre[rows, :].rearrange("(p t) d -> p t d", t=ROW_TILES))
             c_sb.append(c_blk)
 
+        bias_rows = const.tile([P, Z], BF16)
+        nc.gpsimd.memset(bias_rows[:].bitcast(I32), 0)
+
         warm = const.tile([P, 1], F32)
         nc.vector.memset(warm[:], 0.0)
         nc.scalar.activation(out=warm[:], in_=warm[:], func=ACT.Sigmoid)
@@ -70,16 +73,18 @@ def tile_lstmcell_t_e_kernel(tc, x_t, h_pre, c_pre, Wx_words, Wx_scales, bW, Uh,
         nc.vector.memset(spare[:], 0.0)
         w_scales = const.tile([P, X_PASSES, Z], U8, align_bytes=64)
         nc.vector.memset(w_scales[:].rearrange("p c n -> p (c n)").bitcast(I32), 0)
-        bias_rows = const.tile([P, Z], BF16)
-        nc.vector.memset(bias_rows[:], 0.0)
         ident_f32 = const.tile([P, P], F32)
         make_identity(nc, ident_f32[:])
 
         load_h(0)
-        uh_sb = const.tile([P, Z // P, H], BF16)
-        nc.sync.dma_start(out=uh_sb[:], in_=Uh.rearrange("e (a p) k -> p (e a) k", p=P))
         nc.sync.dma_start(out=bias_rows[0:1, :], in_=bW.rearrange("(o e) n -> o (e n)", o=1))
         nc.sync.dma_start(out=bias_rows[1:2, :], in_=bU.rearrange("(o e) n -> o (e n)", o=1))
+        uh_sb = []
+        for half in range(HALVES):
+            uh_half = const.tile([P, N_TILE // P, H], BF16, name="uh_half%d" % half)
+            gates = slice(half * (GATES // HALVES), (half + 1) * (GATES // HALVES))
+            nc.sync.dma_start(out=uh_half[:], in_=Uh[gates].rearrange("e (a p) k -> p (e a) k", p=P))
+            uh_sb.append(uh_half)
         load_x(0)
         w_words = const.tile([P, X_PASSES, Z], U32, align_bytes=64)
         scale_words = Wx_scales.bitcast(I32).rearrange("(e c) q n -> c q e n", c=X_PASSES)
@@ -247,24 +252,24 @@ def tile_lstmcell_t_e_kernel(tc, x_t, h_pre, c_pre, Wx_words, Wx_scales, bW, Uh,
 
         ctx.enter_context(tc.manual_schedule())
 
-        spare_ps = psum_t.tile([P, N_TILE], F32, name="spare_ps", tag="xT_ps1")
+        spare_ps = psum_z.tile([P, N_TILE], F32, name="spare_ps", tag="z_ps")
         for i in range(WARM_UP):
             nc.tensor.matmul(out=spare_ps[:], lhsT=ones[:], rhs=spare[:], start=True, stop=True)
         transpose_h(0)
         uT_sb = const.tile([P, HALVES, H_PASSES, N_TILE], BF16)
-        for gate in range(GATES):
-            uT_ps = psum_z.tile([P, H], F32, name="uT_ps", tag="z_ps")
-            for a in range(H // P):
-                nc.tensor.transpose(uT_ps[:, a * P : (a + 1) * P], uh_sb[:, gate * (H // P) + a, :].bitcast(F32), ident_f32[:])
-            copy = nc.vector.tensor_copy if gate % 2 == 0 else nc.scalar.copy
-            half, place = divmod(gate, GATES // HALVES)
-            copy(out=uT_sb[:, half, :, place * H : (place + 1) * H], in_=uT_ps[:].bitcast(BF16).rearrange("p (n e) -> p e n", e=H_PASSES))
         bias_sb = const.tile([P, Z], F32)
-        bias_ps = [psum_t.tile([P, N_TILE], F32, name="bias_ps0", tag="hT_ps"), psum_z.tile([P, N_TILE], F32, name="bias_ps1", tag="z_ps")]
+        bias_ps = [psum_t.tile([P, N_TILE], F32, name="bias_ps%d" % half, tag="xT_ps%d" % half) for half in range(HALVES)]
+        pair = [nc.vector.tensor_copy, nc.scalar.copy]
         for half in range(HALVES):
-            nc.tensor.matmul(out=bias_ps[half][:], lhsT=ones[:], rhs=bias_rows[:, halves[half]], start=True, stop=True)
-        for half in range(HALVES):
-            nc.scalar.copy(out=bias_sb[:, halves[half]], in_=bias_ps[half][:])
+            for place, copy in enumerate(pair):
+                uT_ps = psum_z.tile([P, H], F32, name="uT_ps", tag="z_ps")
+                for a in range(H // P):
+                    nc.tensor.transpose(uT_ps[:, a * P : (a + 1) * P], uh_sb[half][:, place * (H // P) + a, :].bitcast(F32), ident_f32[:])
+                copy(out=uT_sb[:, half, :, place * H : (place + 1) * H], in_=uT_ps[:].bitcast(BF16).rearrange("p (n e) -> p e n", e=H_PASSES))
+            if half == 0:
+                for side, copy in enumerate(pair):
+                    nc.tensor.matmul(out=bias_ps[side][:], lhsT=ones[:], rhs=bias_rows[:, halves[side]], start=True, stop=True)
+                    copy(out=bias_sb[:, halves[side]], in_=bias_ps[side][:])
 
         whole = slice(0, ROW_TILES)
         first, second = slice(0, 1), slice(1, 2)
@@ -274,29 +279,30 @@ def tile_lstmcell_t_e_kernel(tc, x_t, h_pre, c_pre, Wx_words, Wx_scales, bW, Uh,
                 hidden(b, whole, nc.vector)
             quantise_block(step)
 
-        for step in range(1, BLOCKS):
+        load_block(AHEAD)
+        plain_row_tile(0, 0, 0)
+        quantise_block(0)
+        plain_row_tile(0, 1)
+        sort_block(1)
+        transpose_block(1)
+        mx_row_tile(0, 0)
+        sort_block(2)
+        quantise_block(1)
+        gates_row_tile(0, 0)
+        mx_row_tile(0, 1)
+
+        for step in range(2, BLOCKS):
             a = step - 1
             load_block(a + AHEAD)
-            if step == 1:
-                plain_row_tile(0, 0, 0)
-                quantise_block(0)
-                plain_row_tile(0, 1)
-                sort_block(1)
-                transpose_block(1)
-            else:
-                plain_row_tile(a, 0, step, lambda: shared_port_work(a - 3, step))
-            if exists(a - 1):
-                gates_row_tile(a - 1, 1)
-                cell(a - 1, whole, nc.gpsimd)
+            plain_row_tile(a, 0, step, lambda: shared_port_work(a - 3, step))
+            gates_row_tile(a - 1, 1)
+            cell(a - 1, whole, nc.gpsimd)
             mx_row_tile(a, 0)
             if exists(step + 1):
                 sort_block(step + 1)
-            if step == 1:
-                quantise_block(1)
             if exists(a - 2):
                 tanh_cell(a - 2, whole)
-            if step > 1:
-                plain_row_tile(a, 1)
+            plain_row_tile(a, 1)
             gates_row_tile(a, 0)
             mx_row_tile(a, 1)
 

@@ -26,6 +26,7 @@ HALVES = Z // N_TILE
 ROW_TILES = 2
 BLOCK = ROW_TILES * P
 BLOCKS = B // BLOCK
+HELD = 8
 AHEAD = 4
 WARM_UP = 3
 
@@ -45,12 +46,12 @@ def tile_lstmcell_t_e_kernel(tc, x_t, h_pre, c_pre, Wx_words, Wx_scales, bW, Uh,
         x_sb, h_sb, c_sb = [], [], []
 
         def load_x(b):
-            x_blk = inputs.tile([P, ROW_TILES, D], BF16, name="x_blk")
+            x_blk = inputs.tile([P, ROW_TILES, D], BF16, name="x_blk", bufs=HELD)
             nc.sync.dma_start(out=x_blk[:], in_=x_t[b * BLOCK : (b + 1) * BLOCK, :].rearrange("(p t) d -> p t d", t=ROW_TILES))
             x_sb.append(x_blk)
 
         def load_h(b):
-            h_blk = inputs.tile([P, ROW_TILES, H], BF16, name="h_blk")
+            h_blk = inputs.tile([P, ROW_TILES, H], BF16, name="h_blk", bufs=HELD)
             nc.sync.dma_start(out=h_blk[:], in_=h_pre[b * BLOCK : (b + 1) * BLOCK, :].rearrange("(p t) d -> p t d", t=ROW_TILES))
             h_sb.append(h_blk)
 
@@ -125,7 +126,7 @@ def tile_lstmcell_t_e_kernel(tc, x_t, h_pre, c_pre, Wx_words, Wx_scales, bW, Uh,
                 )
             x_sorted[b] = in_order
 
-        def transpose_x(b, copies):
+        def transpose_x(b):
             grouped = work.tile([P, ROW_TILES, X_PASSES, P, PACK], BF16, align_bytes=64, name="grouped")
             for t in range(ROW_TILES):
                 xT_ps = psum_t.tile([P, X_PASSES, 2, P], F32, name="xT_ps%d" % t)
@@ -136,21 +137,16 @@ def tile_lstmcell_t_e_kernel(tc, x_t, h_pre, c_pre, Wx_words, Wx_scales, bW, Uh,
                 for g in range(X_PASSES):
                     for u in range(2):
                         nc.tensor.transpose(xT_ps[:, g, u, :], words[:, g, u, :], ident_f32[:])
-                copies[t](out=grouped[:, t].bitcast(F32), in_=xT_ps[:].rearrange("p g u r -> p g r u"))
+                nc.scalar.copy(out=grouped[:, t].bitcast(F32), in_=xT_ps[:].rearrange("p g u r -> p g r u"))
             x_grouped[b] = grouped
 
         def transpose_h(b):
             hT_ps = psum_t.tile([P, ROW_TILES, P], F32, name="hT_ps")
             for t in range(ROW_TILES):
                 nc.tensor.transpose(hT_ps[:, t, :], h_sb[b][:, t, :].bitcast(F32), ident_f32[:])
-            hT = work.tile([P, ROW_TILES, P], F32, name="hT")
+            hT = work.tile([P, ROW_TILES, P], F32, name="hT", bufs=4)
             nc.scalar.copy(out=hT[:], in_=hT_ps[:])
             hT_sb[b] = hT
-
-        def transpose_block(b):
-            transpose_x(b, [nc.scalar.copy, nc.scalar.copy])
-            if b > 0:
-                transpose_h(b)
 
         def quantise_block(b):
             codes = work.tile([P, ROW_TILES * X_PASSES * P], U32, align_bytes=64, name="codes")
@@ -164,7 +160,7 @@ def tile_lstmcell_t_e_kernel(tc, x_t, h_pre, c_pre, Wx_words, Wx_scales, bW, Uh,
 
         halves = [slice(half * N_TILE, (half + 1) * N_TILE) for half in range(HALVES)]
 
-        def plain_row_tile(b, t, transposes_of=None, between=None):
+        def plain_row_tile(b, t, transposes=None, between=None):
             if t == 0:
                 z_sb[b] = work.tile([P, ROW_TILES, Z], F32, name="z", bufs=4)
             z = z_sb[b]
@@ -178,17 +174,17 @@ def tile_lstmcell_t_e_kernel(tc, x_t, h_pre, c_pre, Wx_words, Wx_scales, bW, Uh,
                         start=(kt == 0),
                         stop=(kt == H_PASSES - 1),
                     )
-                if half == 0 and transposes_of is not None:
-                    transpose_block(transposes_of)
+                if half == 0 and transposes is not None:
+                    transposes()
             for half in range(HALVES):
                 nc.vector.tensor_tensor(out=z[:, t, halves[half]], in0=zh_ps[half][:], in1=bias_sb[:, halves[half]], op=ALU.add)
                 if half == 0 and between is not None:
                     between()
 
-        def mx_row_tile(b, t):
+        def mx_row_tile(b, t, order=(1, 0)):
             z = z_sb[b]
-            zx_ps = [psum_z.tile([P, N_TILE], F32, name="zx_ps", tag="z_ps") for half in range(HALVES)]
-            for half in range(HALVES):
+            zx_ps = {half: psum_z.tile([P, N_TILE], F32, name="zx_ps", tag="z_ps") for half in order}
+            for half in order:
                 for g in range(X_PASSES):
                     rows = slice((t * X_PASSES + g) * P, (t * X_PASSES + g + 1) * P)
                     nc.tensor.matmul_mx(
@@ -200,7 +196,7 @@ def tile_lstmcell_t_e_kernel(tc, x_t, h_pre, c_pre, Wx_words, Wx_scales, bW, Uh,
                         start=(g == 0),
                         stop=(g == X_PASSES - 1),
                     )
-            for half in range(HALVES):
+            for half in order:
                 nc.vector.tensor_tensor(out=z[:, t, halves[half]], in0=zx_ps[half][:], in1=z[:, t, halves[half]], op=ALU.add)
 
         def matmul_row_tile(b, t, transposes_of=None):
@@ -233,7 +229,7 @@ def tile_lstmcell_t_e_kernel(tc, x_t, h_pre, c_pre, Wx_words, Wx_scales, bW, Uh,
             engine.tensor_tensor(out=ig[:, tiles], in0=z[:, tiles, H : 2 * H], in1=z[:, tiles, 3 * H : Z], op=ALU.mult)
 
         def cell_sum(b, tiles, engine):
-            c_t = block_tile(c_new, b, "c_t")
+            c_t = block_tile(c_new, b, "c_t", bufs=BLOCKS)
             engine.tensor_tensor(out=c_t[:, tiles], in0=fc_sb[b][:, tiles], in1=ig_sb[b][:, tiles], op=ALU.add)
             nc.sync.dma_start(out=out_rows(out_1, b, tiles), in_=c_t[:, tiles])
 
@@ -246,7 +242,7 @@ def tile_lstmcell_t_e_kernel(tc, x_t, h_pre, c_pre, Wx_words, Wx_scales, bW, Uh,
             nc.scalar.activation(out=tanh_c[:, tiles], in_=c_new[b][:, tiles], func=ACT.Tanh)
 
         def hidden(b, tiles, engine):
-            h_t = block_tile(h_new, b, "h_t")
+            h_t = block_tile(h_new, b, "h_t", bufs=BLOCKS)
             engine.tensor_tensor(out=h_t[:, tiles], in0=z_sb[b][:, tiles, 2 * H : 3 * H], in1=tanh_new[b][:, tiles], op=ALU.mult)
             nc.sync.dma_start(out=out_rows(out_0, b, tiles), in_=h_t[:, tiles])
 
@@ -280,42 +276,47 @@ def tile_lstmcell_t_e_kernel(tc, x_t, h_pre, c_pre, Wx_words, Wx_scales, bW, Uh,
             quantise_block(step)
 
         load_block(AHEAD)
-        plain_row_tile(0, 0, 0)
+        plain_row_tile(0, 0, lambda: transpose_x(0))
         quantise_block(0)
         plain_row_tile(0, 1)
         sort_block(1)
-        transpose_block(1)
+        transpose_x(1)
+        transpose_h(1)
         mx_row_tile(0, 0)
         sort_block(2)
         quantise_block(1)
+        plain_row_tile(1, 0, lambda: transpose_h(2))
         gates_row_tile(0, 0)
         mx_row_tile(0, 1)
 
-        for step in range(2, BLOCKS):
-            a = step - 1
-            load_block(a + AHEAD)
-            plain_row_tile(a, 0, step, lambda: shared_port_work(a - 3, step))
-            gates_row_tile(a - 1, 1)
-            cell(a - 1, whole, nc.gpsimd)
-            mx_row_tile(a, 0)
-            if exists(step + 1):
-                sort_block(step + 1)
-            if exists(a - 2):
-                tanh_cell(a - 2, whole)
-            plain_row_tile(a, 1)
-            gates_row_tile(a, 0)
-            mx_row_tile(a, 1)
+        def transposes(b):
+            transpose_x(b)
+            if exists(b + 1):
+                transpose_h(b + 1)
+
+        for b in range(1, BLOCKS - 1):
+            load_block(b + AHEAD)
+            plain_row_tile(b, 1, lambda: transposes(b + 1), lambda: shared_port_work(b - 3, b + 1))
+            gates_row_tile(b - 1, 1)
+            cell(b - 1, whole, nc.gpsimd)
+            mx_row_tile(b, 0)
+            if exists(b + 2):
+                sort_block(b + 2)
+            if exists(b - 2):
+                tanh_cell(b - 2, whole)
+            plain_row_tile(b + 1, 0)
+            gates_row_tile(b, 0)
+            mx_row_tile(b, 1)
 
         last = BLOCKS - 1
+        plain_row_tile(last, 1)
         cell(last - 1, first, nc.gpsimd)
         gates_row_tile(last - 1, 1)
         cell_products(last - 1, second, nc.gpsimd)
-        plain_row_tile(last, 0)
         tanh_cell(last - 2, whole)
         mx_row_tile(last, 0)
-        plain_row_tile(last, 1)
         gates_row_tile(last, 0)
-        mx_row_tile(last, 1)
+        mx_row_tile(last, 1, range(HALVES))
         hidden(last - 3, whole, nc.vector)
         cell_sum(last - 1, second, nc.vector)
         cell_products(last, first, nc.vector)

@@ -160,24 +160,33 @@ def tile_lstmcell_t_e_kernel(tc, x_t, h_pre, c_pre, Wx_words, Wx_scales, bW, Uh,
 
         halves = [slice(half * N_TILE, (half + 1) * N_TILE) for half in range(HALVES)]
 
+        def left_to_scalar(b, t, half):
+            return b == BLOCKS - 1 and t == 1 and half == 0
+
         def plain_row_tile(b, t, transposes=None, between=None):
             if t == 0:
                 z_sb[b] = work.tile([P, ROW_TILES, Z], F32, name="z", bufs=4)
             z = z_sb[b]
             zh_ps = [psum_z.tile([P, N_TILE], F32, name="zh_ps", tag="z_ps") for half in range(HALVES)]
             for half in range(HALVES):
+                by_scalar = left_to_scalar(b, t, half)
                 for kt in range(H_PASSES):
                     nc.tensor.matmul(
                         out=zh_ps[half][:],
                         lhsT=hT_sb[b][:, t, :].bitcast(BF16).rearrange("p (r e) -> p e r", e=H_PASSES)[:, kt, :],
                         rhs=uT_sb[:, half, kt, :],
                         start=(kt == 0),
-                        stop=(kt == H_PASSES - 1),
+                        stop=(kt == H_PASSES - 1 and not by_scalar),
                     )
+                if by_scalar:
+                    nc.tensor.matmul(out=zh_ps[half][:], lhsT=ones[:], rhs=bias_rows[:, halves[half]], start=False, stop=True)
                 if half == 0 and transposes is not None:
                     transposes()
             for half in range(HALVES):
-                nc.vector.tensor_tensor(out=z[:, t, halves[half]], in0=zh_ps[half][:], in1=bias_sb[:, halves[half]], op=ALU.add)
+                if left_to_scalar(b, t, half):
+                    nc.scalar.copy(out=z[:, t, halves[half]], in_=zh_ps[half][:])
+                else:
+                    nc.vector.tensor_tensor(out=z[:, t, halves[half]], in0=zh_ps[half][:], in1=bias_sb[:, halves[half]], op=ALU.add)
                 if half == 0 and between is not None:
                     between()
 
@@ -198,10 +207,6 @@ def tile_lstmcell_t_e_kernel(tc, x_t, h_pre, c_pre, Wx_words, Wx_scales, bW, Uh,
                     )
             for half in order:
                 nc.vector.tensor_tensor(out=z[:, t, halves[half]], in0=zx_ps[half][:], in1=z[:, t, halves[half]], op=ALU.add)
-
-        def matmul_row_tile(b, t, transposes_of=None):
-            plain_row_tile(b, t, transposes_of)
-            mx_row_tile(b, t)
 
         def gates_row_tile(b, t, bank_by_bank=False):
             z = z_sb[b]
@@ -312,22 +317,22 @@ def tile_lstmcell_t_e_kernel(tc, x_t, h_pre, c_pre, Wx_words, Wx_scales, bW, Uh,
         plain_row_tile(last, 1)
         cell(last - 1, first, nc.gpsimd)
         gates_row_tile(last - 1, 1)
-        cell_products(last - 1, second, nc.gpsimd)
         tanh_cell(last - 2, whole)
         mx_row_tile(last, 0)
         gates_row_tile(last, 0)
         mx_row_tile(last, 1, range(HALVES))
         hidden(last - 3, whole, nc.vector)
-        cell_sum(last - 1, second, nc.vector)
+        cell_products(last - 1, second, nc.vector)
         cell_products(last, first, nc.vector)
-        hidden(last - 2, whole, nc.vector)
+        cell_sum(last - 1, second, nc.vector)
+        cell_sum(last, first, nc.vector)
         gates_row_tile(last, 1, bank_by_bank=True)
         tanh_cell(last - 1, whole)
-        cell_sum(last, first, nc.vector)
         tanh_cell(last, first)
         cell_products(last, second, nc.vector)
-        hidden(last - 1, whole, nc.vector)
+        hidden(last - 2, whole, nc.vector)
         cell_sum(last, second, nc.vector)
         tanh_cell(last, second)
+        hidden(last - 1, whole, nc.vector)
         hidden(last, first, nc.vector)
         hidden(last, second, nc.vector)

from contextlib import ExitStack

import concourse.mybir as mybir
from concourse.masks import make_identity

F32 = mybir.dt.float32
BF16 = mybir.dt.bfloat16
I32 = mybir.dt.int32
U32 = mybir.dt.uint32
U8 = mybir.dt.uint8
FP8X4 = mybir.dt.float8_e4m3fn_x4
ACT = mybir.ActivationFunctionType
ALU = mybir.AluOpType

B, D, H, GATES = 4096, 1024, 256, 4
FLOPS = 2 * B * D * GATES * H + 2 * B * H * GATES * H

P = 128
PACK = 4
K_PASS = P * PACK
X_PASSES = D // K_PASS
H_PASSES = H // P
Z = GATES * H
N_TILE = 512
HALVES = Z // N_TILE
ROW_TILES = 2
BLOCK = ROW_TILES * P
BLOCKS = B // BLOCK
HELD = 8
AHEAD = 4
WARM_UP = 3


def tile_lstmcell_t_e_kernel(tc, x_t, h_pre, c_pre, Wx_words, Wx_scales, bW, Uh, bU, out_0, out_1):
    nc = tc.nc
    with ExitStack() as ctx:
        const = ctx.enter_context(tc.tile_pool(name="const", bufs=1))
        inputs = ctx.enter_context(tc.tile_pool(name="inputs", bufs=BLOCKS))
        work = ctx.enter_context(tc.tile_pool(name="work", bufs=3))
        psum_t = ctx.enter_context(tc.psum_pool(name="psum_t", bufs=1))
        psum_z = ctx.enter_context(tc.psum_pool(name="psum_z", bufs=5))

        def exists(b):
            return 0 <= b < BLOCKS

        x_sb, h_sb, c_sb = [], [], []

        def load_x(b):
            x_blk = inputs.tile([P, ROW_TILES, D], BF16, name="x_blk", bufs=HELD)
            nc.sync.dma_start(out=x_blk[:], in_=x_t[b * BLOCK : (b + 1) * BLOCK, :].rearrange("(p t) d -> p t d", t=ROW_TILES))
            x_sb.append(x_blk)

        def load_h(b):
            h_blk = inputs.tile([P, ROW_TILES, H], BF16, name="h_blk", bufs=HELD)
            nc.sync.dma_start(out=h_blk[:], in_=h_pre[b * BLOCK : (b + 1) * BLOCK, :].rearrange("(p t) d -> p t d", t=ROW_TILES))
            h_sb.append(h_blk)

        def load_c(b):
            rows = slice(b * BLOCK, (b + 1) * BLOCK)
            c_blk = inputs.tile([P, ROW_TILES, H], BF16, name="c_blk")
            nc.sync.dma_start(out=c_blk[:], in_=c_pre[rows, :].rearrange("(p t) d -> p t d", t=ROW_TILES))
            c_sb.append(c_blk)

        bias_rows = const.tile([P, Z], BF16)
        nc.gpsimd.memset(bias_rows[:].bitcast(I32), 0)

        warm = const.tile([P, 1], F32)
        nc.vector.memset(warm[:], 0.0)
        nc.scalar.activation(out=warm[:], in_=warm[:], func=ACT.Sigmoid)

        ones = const.tile([P, P], BF16)
        nc.vector.memset(ones[:], 1.0)
        spare = const.tile([P, N_TILE], BF16)
        nc.vector.memset(spare[:], 0.0)
        w_scales = const.tile([P, X_PASSES, Z], U8, align_bytes=64)
        nc.vector.memset(w_scales[:].rearrange("p c n -> p (c n)").bitcast(I32), 0)
        ident_f32 = const.tile([P, P], F32)
        make_identity(nc, ident_f32[:])

        load_h(0)
        nc.sync.dma_start(out=bias_rows[0:1, :], in_=bW.rearrange("(o e) n -> o (e n)", o=1))
        nc.sync.dma_start(out=bias_rows[1:2, :], in_=bU.rearrange("(o e) n -> o (e n)", o=1))
        uh_sb = []
        for half in range(HALVES):
            uh_half = const.tile([P, N_TILE // P, H], BF16, name="uh_half%d" % half)
            gates = slice(half * (GATES // HALVES), (half + 1) * (GATES // HALVES))
            nc.sync.dma_start(out=uh_half[:], in_=Uh[gates].rearrange("e (a p) k -> p (e a) k", p=P))
            uh_sb.append(uh_half)
        load_x(0)
        w_words = const.tile([P, X_PASSES, Z], U32, align_bytes=64)
        scale_words = Wx_scales.bitcast(I32).rearrange("(e c) q n -> c q e n", c=X_PASSES)
        code_words = Wx_words.rearrange("g p n t -> g p (n t)").bitcast(I32).rearrange("(e c) p n -> c p e n", c=X_PASSES)
        for c in range(X_PASSES):
            for quad in range(4):
                nc.sync.dma_start(
                    out=w_scales[32 * quad : 32 * quad + 4, c, :].bitcast(I32).rearrange("q (e n) -> q e n", e=GATES),
                    in_=scale_words[c, 4 * quad : 4 * quad + 4],
                )
            if c == 0:
                load_x(1)
                load_h(1)
        for c in range(X_PASSES):
            nc.sync.dma_start(
                out=w_words[:, c, :].bitcast(I32).rearrange("p (e n) -> p e n", e=GATES),
                in_=code_words[c],
            )
        def load_block(b):
            if exists(b):
                load_x(b)
                load_h(b)
            if exists(b - 2):
                load_c(b - 2)

        for b in range(2, AHEAD):
            load_block(b)

        x_sorted, x_grouped, x_codes, x_scales, hT_sb, z_sb = {}, {}, {}, {}, {}, {}
        fc_sb, ig_sb, c_new, tanh_new, h_new = {}, {}, {}, {}, {}

        def sort_block(b):
            in_order = work.tile([P, ROW_TILES, X_PASSES, 2, P], F32, name="in_order")
            for t in range(ROW_TILES):
                nc.scalar.copy(
                    out=in_order[:, t],
                    in_=x_sb[b][:, t, :].bitcast(F32).rearrange("p (g j u) -> p g u j", g=X_PASSES, u=2),
                )
            x_sorted[b] = in_order

        def transpose_x(b):
            grouped = work.tile([P, ROW_TILES, X_PASSES, P, PACK], BF16, align_bytes=64, name="grouped")
            for t in range(ROW_TILES):
                xT_ps = psum_t.tile([P, X_PASSES, 2, P], F32, name="xT_ps%d" % t)
                if b in x_sorted:
                    words = x_sorted[b][:, t]
                else:
                    words = x_sb[b][:, t, :].bitcast(F32).rearrange("p (g j u) -> p g u j", g=X_PASSES, u=2)
                for g in range(X_PASSES):
                    for u in range(2):
                        nc.tensor.transpose(xT_ps[:, g, u, :], words[:, g, u, :], ident_f32[:])
                nc.scalar.copy(out=grouped[:, t].bitcast(F32), in_=xT_ps[:].rearrange("p g u r -> p g r u"))
            x_grouped[b] = grouped

        def transpose_h(b):
            hT_ps = psum_t.tile([P, ROW_TILES, P], F32, name="hT_ps")
            for t in range(ROW_TILES):
                nc.tensor.transpose(hT_ps[:, t, :], h_sb[b][:, t, :].bitcast(F32), ident_f32[:])
            hT = work.tile([P, ROW_TILES, P], F32, name="hT", bufs=4)
            nc.scalar.copy(out=hT[:], in_=hT_ps[:])
            hT_sb[b] = hT

        def quantise_block(b):
            codes = work.tile([P, ROW_TILES * X_PASSES * P], U32, align_bytes=64, name="codes")
            scales = work.tile([P, ROW_TILES * X_PASSES * P], U8, align_bytes=64, name="scales")
            nc.vector.quantize_mx(
                out=codes[:].bitcast(FP8X4),
                scales=scales[:],
                in_=x_grouped[b][:].rearrange("p t g r k -> p (t g r k)"),
            )
            x_codes[b], x_scales[b] = codes, scales

        halves = [slice(half * N_TILE, (half + 1) * N_TILE) for half in range(HALVES)]

        def left_to_scalar(b, t, half):
            return b == BLOCKS - 1 and t == 1 and half == 0

        def plain_row_tile(b, t, transposes=None, between=None):
            if t == 0:
                z_sb[b] = work.tile([P, ROW_TILES, Z], F32, name="z", bufs=4)
            z = z_sb[b]
            zh_ps = [psum_z.tile([P, N_TILE], F32, name="zh_ps", tag="z_ps") for half in range(HALVES)]
            for half in range(HALVES):
                by_scalar = left_to_scalar(b, t, half)
                for kt in range(H_PASSES):
                    nc.tensor.matmul(
                        out=zh_ps[half][:],
                        lhsT=hT_sb[b][:, t, :].bitcast(BF16).rearrange("p (r e) -> p e r", e=H_PASSES)[:, kt, :],
                        rhs=uT_sb[:, half, kt, :],
                        start=(kt == 0),
                        stop=(kt == H_PASSES - 1 and not by_scalar),
                    )
                if by_scalar:
                    nc.tensor.matmul(out=zh_ps[half][:], lhsT=ones[:], rhs=bias_rows[:, halves[half]], start=False, stop=True)
                if half == 0 and transposes is not None:
                    transposes()
            for half in range(HALVES):
                if left_to_scalar(b, t, half):
                    nc.scalar.copy(out=z[:, t, halves[half]], in_=zh_ps[half][:])
                else:
                    nc.vector.tensor_tensor(out=z[:, t, halves[half]], in0=zh_ps[half][:], in1=bias_sb[:, halves[half]], op=ALU.add)
                if half == 0 and between is not None:
                    between()

        def mx_row_tile(b, t, order=(1, 0)):
            z = z_sb[b]
            zx_ps = {half: psum_z.tile([P, N_TILE], F32, name="zx_ps", tag="z_ps") for half in order}
            for half in order:
                for g in range(X_PASSES):
                    rows = slice((t * X_PASSES + g) * P, (t * X_PASSES + g + 1) * P)
                    nc.tensor.matmul_mx(
                        out=zx_ps[half][:],
                        lhsT=x_codes[b][:, rows].bitcast(FP8X4),
                        lhsT_scale=x_scales[b][:, rows],
                        rhs=w_words[:, g, halves[half]].bitcast(FP8X4),
                        rhs_scale=w_scales[:, g, halves[half]],
                        start=(g == 0),
                        stop=(g == X_PASSES - 1),
                    )
            for half in order:
                nc.vector.tensor_tensor(out=z[:, t, halves[half]], in0=zx_ps[half][:], in1=z[:, t, halves[half]], op=ALU.add)

        def gates_row_tile(b, t, bank_by_bank=False):
            z = z_sb[b]
            if bank_by_bank:
                nc.scalar.activation(out=z[:, t, 0 : 2 * H], in_=z[:, t, 0 : 2 * H], func=ACT.Sigmoid)
                nc.scalar.activation(out=z[:, t, 3 * H : Z], in_=z[:, t, 3 * H : Z], func=ACT.Tanh)
                nc.scalar.activation(out=z[:, t, 2 * H : 3 * H], in_=z[:, t, 2 * H : 3 * H], func=ACT.Sigmoid)
            else:
                nc.scalar.activation(out=z[:, t, 0 : 3 * H], in_=z[:, t, 0 : 3 * H], func=ACT.Sigmoid)
                nc.scalar.activation(out=z[:, t, 3 * H : Z], in_=z[:, t, 3 * H : Z], func=ACT.Tanh)

        def block_tile(kept, b, name, bufs=3):
            if b not in kept:
                kept[b] = work.tile([P, ROW_TILES, H], F32, name=name, bufs=bufs)
            return kept[b]

        def out_rows(out, b, tiles):
            return out[b * BLOCK : (b + 1) * BLOCK, :].rearrange("(p t) n -> p t n", t=ROW_TILES)[:, tiles, :]

        def cell_products(b, tiles, engine):
            z = z_sb[b]
            fc = block_tile(fc_sb, b, "fc")
            engine.tensor_tensor(out=fc[:, tiles], in0=z[:, tiles, 0:H], in1=c_sb[b][:, tiles], op=ALU.mult)
            ig = block_tile(ig_sb, b, "ig")
            engine.tensor_tensor(out=ig[:, tiles], in0=z[:, tiles, H : 2 * H], in1=z[:, tiles, 3 * H : Z], op=ALU.mult)

        def cell_sum(b, tiles, engine):
            c_t = block_tile(c_new, b, "c_t", bufs=BLOCKS)
            engine.tensor_tensor(out=c_t[:, tiles], in0=fc_sb[b][:, tiles], in1=ig_sb[b][:, tiles], op=ALU.add)
            nc.sync.dma_start(out=out_rows(out_1, b, tiles), in_=c_t[:, tiles])

        def cell(b, tiles, engine):
            cell_products(b, tiles, engine)
            cell_sum(b, tiles, engine)

        def tanh_cell(b, tiles):
            tanh_c = block_tile(tanh_new, b, "tanh_c", bufs=4)
            nc.scalar.activation(out=tanh_c[:, tiles], in_=c_new[b][:, tiles], func=ACT.Tanh)

        def hidden(b, tiles, engine):
            h_t = block_tile(h_new, b, "h_t", bufs=BLOCKS)
            engine.tensor_tensor(out=h_t[:, tiles], in0=z_sb[b][:, tiles, 2 * H : 3 * H], in1=tanh_new[b][:, tiles], op=ALU.mult)
            nc.sync.dma_start(out=out_rows(out_0, b, tiles), in_=h_t[:, tiles])

        ctx.enter_context(tc.manual_schedule())

        spare_ps = psum_z.tile([P, N_TILE], F32, name="spare_ps", tag="z_ps")
        for i in range(WARM_UP):
            nc.tensor.matmul(out=spare_ps[:], lhsT=ones[:], rhs=spare[:], start=True, stop=True)
        transpose_h(0)
        uT_sb = const.tile([P, HALVES, H_PASSES, N_TILE], BF16)
        bias_sb = const.tile([P, Z], F32)
        bias_ps = [psum_t.tile([P, N_TILE], F32, name="bias_ps%d" % half, tag="xT_ps%d" % half) for half in range(HALVES)]
        pair = [nc.vector.tensor_copy, nc.scalar.copy]
        for half in range(HALVES):
            for place, copy in enumerate(pair):
                uT_ps = psum_z.tile([P, H], F32, name="uT_ps", tag="z_ps")
                for a in range(H // P):
                    nc.tensor.transpose(uT_ps[:, a * P : (a + 1) * P], uh_sb[half][:, place * (H // P) + a, :].bitcast(F32), ident_f32[:])
                copy(out=uT_sb[:, half, :, place * H : (place + 1) * H], in_=uT_ps[:].bitcast(BF16).rearrange("p (n e) -> p e n", e=H_PASSES))
            if half == 0:
                for side, copy in enumerate(pair):
                    nc.tensor.matmul(out=bias_ps[side][:], lhsT=ones[:], rhs=bias_rows[:, halves[side]], start=True, stop=True)
                    copy(out=bias_sb[:, halves[side]], in_=bias_ps[side][:])

        whole = slice(0, ROW_TILES)
        first, second = slice(0, 1), slice(1, 2)

        def shared_port_work(b, step):
            if exists(b):
                hidden(b, whole, nc.vector)
            quantise_block(step)

        load_block(AHEAD)
        plain_row_tile(0, 0, lambda: transpose_x(0))
        quantise_block(0)
        plain_row_tile(0, 1)
        sort_block(1)
        transpose_x(1)
        transpose_h(1)
        mx_row_tile(0, 0)
        sort_block(2)
        quantise_block(1)
        plain_row_tile(1, 0, lambda: transpose_h(2))
        gates_row_tile(0, 0)
        mx_row_tile(0, 1)

        def transposes(b):
            transpose_x(b)
            if exists(b + 1):
                transpose_h(b + 1)

        for b in range(1, BLOCKS - 1):
            load_block(b + AHEAD)
            plain_row_tile(b, 1, lambda: transposes(b + 1), lambda: shared_port_work(b - 3, b + 1))
            gates_row_tile(b - 1, 1)
            cell(b - 1, whole, nc.gpsimd)
            mx_row_tile(b, 0)
            if exists(b + 2):
                sort_block(b + 2)
            if exists(b - 2):
                tanh_cell(b - 2, whole)
            plain_row_tile(b + 1, 0)
            gates_row_tile(b, 0)
            mx_row_tile(b, 1)

        last = BLOCKS - 1
        plain_row_tile(last, 1)
        cell(last - 1, first, nc.gpsimd)
        gates_row_tile(last - 1, 1)
        tanh_cell(last - 2, whole)
        mx_row_tile(last, 0)
        gates_row_tile(last, 0)
        mx_row_tile(last, 1, range(HALVES))
        hidden(last - 3, whole, nc.vector)
        cell_products(last - 1, second, nc.vector)
        cell_products(last, first, nc.vector)
        cell_sum(last - 1, second, nc.vector)
        cell_sum(last, first, nc.vector)
        gates_row_tile(last, 1, bank_by_bank=True)
        tanh_cell(last - 1, whole)
        tanh_cell(last, first)
        cell_products(last, second, nc.vector)
        hidden(last - 2, whole, nc.vector)
        cell_sum(last, second, nc.vector)
        tanh_cell(last, second)
        hidden(last - 1, whole, nc.vector)
        hidden(last, first, nc.vector)
        hidden(last, second, nc.vector)
